import numpy as np
import ml_dtypes


def mxq(x, axis, fmt="e4m3"):
    dtype, down = {"e4m3": (ml_dtypes.float8_e4m3fn, 7), "e5m2": (ml_dtypes.float8_e5m2, 14)}[fmt]
    v = np.moveaxis(np.asarray(x, np.float32).astype(ml_dtypes.bfloat16).astype(np.float64), axis, -1)
    blocks = v.reshape(v.shape[:-1] + (-1, 32))
    amax = np.abs(blocks).max(-1, keepdims=True)
    byte = np.maximum(np.where(amax > 0, np.frexp(amax)[1] - 1 + 127, 0) - down, 1)
    scale = np.exp2(byte - 127.0)
    codes = (blocks / scale).astype(np.float32).astype(dtype).astype(np.float64)
    return np.moveaxis((codes * scale).reshape(v.shape), -1, axis)


WIDE = False


def mx_kscale(k):
    if not WIDE:
        return np.ones(k)
    levels = np.array([10, -10, 5, -5, 0])
    if k % 512:
        return np.exp2(np.random.permutation(np.resize(levels, k // 32))).repeat(32)
    a = np.empty((k // 512, 16))
    for p in range(k // 512):
        a[p, :8] = np.random.permutation(np.resize(levels, 8))
        for g in range(8):
            far = levels[np.abs(levels - a[p, g]) >= 10]
            a[p, g + 8] = far[np.random.randint(len(far))]
    return np.exp2(a.ravel()).repeat(32)


BF16 = ml_dtypes.bfloat16


def bf(x):
    return np.asarray(x, np.float32).astype(BF16)


def f64(x):
    return np.asarray(x).astype(np.float64)


B, T, C = 4, 1024, 512


def setup_inputs():
    a = np.log2(mx_kscale(T))
    A = float(a.max() - a.min())
    wide = float(A > 0)
    small = a < 0.5 * (a.max() + a.min())
    z = np.random.standard_normal((B, T, C))
    if wide:
        z = z / np.sqrt(np.mean(z * z, axis=-1, keepdims=True))
    r = bf((1.28 / C) * (1.0 + 0.05 * np.random.standard_normal(1)) + A * np.log(2.0) / C)
    rho = float(f64(r)[0]) * C * wide
    row = np.where(small, np.exp(-rho), 1.0)
    return {"x": bf(z * row[None, :, None]),
            "r_sigma": r,
            "margin": bf(-0.4 + 0.1 * np.random.standard_normal(1) + rho)}


def reference(x, r_sigma, margin):
    x, r_sigma, margin = f64(x), f64(r_sigma), f64(margin)
    _, size, _ = x.shape
    sq = np.sum(x * x, axis=-1)
    gram = x @ x.transpose(0, 2, 1)
    sqdist = np.maximum(sq[:, :, None] + sq[:, None, :] - 2.0 * gram, 0.0)
    Kmat = np.exp(-sqdist * r_sigma[0] + margin[0])
    Kmat = Kmat * (1.0 - np.eye(size))
    return x + (mxq(Kmat, 2, "e4m3") @ mxq(x, 1, "e4m3"))

@@ -1,0 +1,180 @@
+from contextlib import ExitStack
+
+import concourse.mybir as mybir
+from concourse.masks import make_identity
+
+BF16 = mybir.dt.bfloat16
+F32 = mybir.dt.float32
+U32 = mybir.dt.uint32
+U8 = mybir.dt.uint8
+FP8X4 = mybir.dt.float8_e4m3fn_x4
+ALU = mybir.AluOpType
+ACT = mybir.ActivationFunctionType
+
+B, T, C = 4, 1024, 512
+P = 128
+NT = T // P
+KC = C // P
+PACK = 4
+NG = T // (P * PACK)
+BANK = 512
+
+FLOPS = 2 * (2 * B * T * T * C)
+
+
+def tile_k_attention_ex_t_kernel(tc, x, r_sigma, margin, out):
+    nc = tc.nc
+    with ExitStack() as ctx:
+        const = ctx.enter_context(tc.tile_pool(name="const", bufs=1))
+        xin = ctx.enter_context(tc.tile_pool(name="xin", bufs=B))
+        two = ctx.enter_context(tc.tile_pool(name="two", bufs=2))
+        three = ctx.enter_context(tc.tile_pool(name="three", bufs=3))
+        four = ctx.enter_context(tc.tile_pool(name="four", bufs=4))
+        psum_g = ctx.enter_context(tc.psum_pool(name="psum_g", bufs=3))
+        psum_t = ctx.enter_context(tc.psum_pool(name="psum_t", bufs=3))
+        psum_o = ctx.enter_context(tc.psum_pool(name="psum_o", bufs=2))
+
+        r_bf = const.tile([P, 1], BF16)
+        m_bf = const.tile([P, 1], BF16)
+        nc.scalar.dma_start(out=r_bf[:], in_=r_sigma.partition_broadcast(P))
+        nc.scalar.dma_start(out=m_bf[:], in_=margin.partition_broadcast(P))
+
+        x_tok = x.rearrange("b (g p j) c -> b g p j c", p=P, j=PACK)
+        out_tok = out.rearrange("b (g p j) c -> b g p j c", p=P, j=PACK)
+
+        x_sb = []
+        for b in range(B):
+            xb = xin.tile([P, NT, C], BF16, name="xb", tag="xb")
+            for h in range(2):
+                nc.sync.dma_start(out=xb[:, PACK * h : PACK * h + PACK, :], in_=x_tok[b, h])
+            x_sb.append(xb)
+
+        ident_bf = const.tile([P, P], BF16)
+        make_identity(nc, ident_bf[:])
+        ident_f = const.tile([P, P], F32)
+        make_identity(nc, ident_f[:])
+        offdiag = const.tile([P, P], BF16)
+        nc.vector.tensor_scalar(out=offdiag[:], in0=ident_bf[:], scalar1=-1.0, scalar2=1.0, op0=ALU.mult, op1=ALU.add)
+
+        two_r = const.tile([P, 1], F32)
+        nc.vector.tensor_scalar(out=two_r[:], in0=r_bf[:], scalar1=2.0, scalar2=None, op0=ALU.mult)
+        m_f = const.tile([P, 1], F32)
+        nc.vector.tensor_copy(out=m_f[:], in_=m_bf[:])
+        e_m = const.tile([P, 1], F32)
+        nc.scalar.activation(out=e_m[:], in_=m_f[:], func=ACT.Exp)
+
+        state = {}
+
+        def prep(b):
+            xb = x_sb[b]
+            sq = two.tile([P, NT], F32, name="sq", tag="sq")
+            for a in range(NT):
+                junk = two.tile([P, C], BF16, name="junk", tag="junk")
+                nc.scalar.activation(out=junk[:], in_=xb[:, a, :], func=ACT.Square, accum_out=sq[:, a : a + 1])
+            nhsq = two.tile([P, NT], F32, name="nhsq", tag="nhsq")
+            nc.vector.tensor_scalar(out=nhsq[:], in0=sq[:], scalar1=-0.5, scalar2=None, op0=ALU.mult)
+
+            xT = two.tile([P, KC, T], BF16, name="xT", tag="xT")
+            for a in range(NT):
+                tp = psum_t.tile([P, KC, P], BF16, name="tp", tag="tr")
+                for k in range(KC):
+                    nc.tensor.transpose(tp[:, k, :], xb[:, a, P * k : P * k + P], ident_bf[:])
+                nc.scalar.copy(out=xT[:, :, P * a : P * a + P], in_=tp[:])
+
+            nhsqt = two.tile([P, T], F32, name="nhsqt", tag="nhsqt")
+            for h in range(T // BANK):
+                bc = psum_t.tile([P, BANK], F32, name="bc", tag="tr")
+                for i in range(BANK // P):
+                    a = h * (BANK // P) + i
+                    nc.tensor.transpose(bc[:, P * i : P * i + P], nhsq[:, a : a + 1].to_broadcast([P, P]), ident_f[:])
+                nc.scalar.copy(out=nhsqt[:, BANK * h : BANK * h + BANK], in_=bc[:])
+
+            xg = two.tile([P, NG, C, PACK], BF16, name="xg", tag="xg", align_bytes=64)
+            xq = two.tile([P, NG, C], U32, name="xq", tag="xq", align_bytes=64)
+            xs = two.tile([P, NG, C], U8, name="xs", tag="xs", align_bytes=64)
+            for g in range(NG):
+                nc.vector.tensor_copy(
+                    out=xg[:, g].rearrange("p (c i) j -> p c j i", i=4),
+                    in_=xb[:, PACK * g : PACK * g + PACK, :].rearrange("p j (c i) -> p c j i", i=4),
+                )
+            for g in range(NG):
+                nc.vector.quantize_mx(
+                    out=xq[:, g, :].bitcast(FP8X4),
+                    scales=xs[:, g, :],
+                    in_=xg[:, g].rearrange("p c j -> p (c j)"),
+                )
+            kc = two.tile([P, NT, T], BF16, name="kc", tag="kc")
+            kq = two.tile([P, NT, NG, P], U32, name="kq", tag="kq", align_bytes=64)
+            ks = two.tile([P, NT, NG, P], U8, name="ks", tag="ks", align_bytes=64)
+            state[b] = (nhsq, xT, nhsqt, xq, xs, kc, kq, ks)
+
+        def row(b, a):
+            xb = x_sb[b]
+            nhsq, xT, nhsqt, xq, xs, kc, kq, ks = state[b]
+            lo = P * a
+            z = three.tile([P, T], F32, name="z", tag="z")
+            c0 = lo
+            while c0 < T:
+                w = min(BANK, T - c0)
+                gp = psum_g.tile([P, BANK], F32, name="gp", tag="g")
+                for k in range(KC):
+                    nc.tensor.matmul(
+                        gp[:, :w], lhsT=xT[:, k, lo : lo + P], rhs=xT[:, k, c0 : c0 + w],
+                        start=(k == 0), stop=(k == KC - 1),
+                    )
+                nc.vector.scalar_tensor_tensor(
+                    out=z[:, c0 : c0 + w], in0=gp[:, :w], scalar=nhsq[:, a : a + 1], in1=nhsqt[:, c0 : c0 + w],
+                    op0=ALU.add, op1=ALU.add,
+                )
+                c0 += w
+            nc.scalar.activation(out=kc[:, a, lo:T], in_=z[:, lo:T], func=ACT.Exp, bias=m_f[:], scale=two_r[:])
+            nc.vector.tensor_tensor(out=kc[:, a, lo : lo + P], in0=kc[:, a, lo : lo + P], in1=offdiag[:], op=ALU.mult)
+            if a < PACK:
+                nc.vector.tensor_scalar(
+                    out=kc[:, a, BANK:T], in0=kc[:, a, BANK:T], scalar1=e_m[:], scalar2=None, op0=ALU.min
+                )
+            kt = None
+            if a < NT - 1:
+                kt = psum_t.tile([P, NT, P], BF16, name="kt", tag="tr")
+                for s in range(a + 1, NT):
+                    nc.tensor.transpose(kt[:, s, :], kc[:, a, P * s : P * s + P], ident_bf[:])
+            grp = four.tile([P, NG, P, PACK], BF16, name="grp", tag="grp", align_bytes=64)
+            for g in range(NG):
+                nd = max(0, min(PACK, a - PACK * g + 1))
+                if nd > 0:
+                    nc.vector.tensor_scalar(
+                        out=grp[:, g, :, 0:nd],
+                        in0=kc[:, PACK * g : PACK * g + nd, lo : lo + P].rearrange("p j t -> p t j"),
+                        scalar1=e_m[:], scalar2=None, op0=ALU.min,
+                    )
+                if nd == 0:
+                    nc.scalar.copy(out=grp[:, g], in_=kt[:, PACK * g : PACK * g + PACK, :].rearrange("p j t -> p t j"))
+                elif nd < PACK:
+                    nc.vector.tensor_scalar(
+                        out=grp[:, g, :, nd:PACK],
+                        in0=kt[:, PACK * g + nd : PACK * g + PACK, :].rearrange("p j t -> p t j"),
+                        scalar1=e_m[:], scalar2=None, op0=ALU.min,
+                    )
+            nc.vector.quantize_mx(
+                out=kq[:, a].rearrange("p g t -> p (g t)").bitcast(FP8X4),
+                scales=ks[:, a].rearrange("p g t -> p (g t)"),
+                in_=grp[:].rearrange("p g t j -> p (g t j)"),
+            )
+            op = psum_o.tile([P, C], F32, name="op", tag="o")
+            for g in range(NG):
+                nc.tensor.matmul_mx(
+                    out=op[:],
+                    lhsT=kq[:, a, g, :].bitcast(FP8X4), lhsT_scale=ks[:, a, g, :],
+                    rhs=xq[:, g, :].bitcast(FP8X4), rhs_scale=xs[:, g, :],
+                    start=(g == 0), stop=(g == NG - 1),
+                )
+            res = four.tile([P, C], F32, name="res", tag="res")
+            nc.vector.tensor_tensor(out=res[:], in0=op[:], in1=xb[:, a, :], op=ALU.add)
+            nc.sync.dma_start(out=out_tok[b, a // PACK, :, a % PACK, :], in_=res[:])
+
+        prep(0)
+        for b in range(B):
+            for a in range(NT):
+                row(b, a)
+                if a == 2 and b + 1 < B:
+                    prep(b + 1)

@@ -18,6 +18,8 @@ KC = C // P
 PACK = 4
 NG = T // (P * PACK)
 BANK = 512
+LEAD = 2
+HEAD = 3
 
 FLOPS = 2 * (2 * B * T * T * C)
 
@@ -28,153 +30,258 @@ def tile_k_attention_ex_t_kernel(tc, x, r_sigma, margin, out):
         const = ctx.enter_context(tc.tile_pool(name="const", bufs=1))
         xin = ctx.enter_context(tc.tile_pool(name="xin", bufs=B))
         two = ctx.enter_context(tc.tile_pool(name="two", bufs=2))
-        three = ctx.enter_context(tc.tile_pool(name="three", bufs=3))
         four = ctx.enter_context(tc.tile_pool(name="four", bufs=4))
-        psum_g = ctx.enter_context(tc.psum_pool(name="psum_g", bufs=3))
-        psum_t = ctx.enter_context(tc.psum_pool(name="psum_t", bufs=3))
+        psum_w = ctx.enter_context(tc.psum_pool(name="psum_w", bufs=6))
         psum_o = ctx.enter_context(tc.psum_pool(name="psum_o", bufs=2))
 
-        r_bf = const.tile([P, 1], BF16)
-        m_bf = const.tile([P, 1], BF16)
+        r_bf = const.tile([P, 1], BF16, name="r_bf")
+        m_bf = const.tile([P, 1], BF16, name="m_bf")
         nc.scalar.dma_start(out=r_bf[:], in_=r_sigma.partition_broadcast(P))
         nc.scalar.dma_start(out=m_bf[:], in_=margin.partition_broadcast(P))
 
         x_tok = x.rearrange("b (g p j) c -> b g p j c", p=P, j=PACK)
         out_tok = out.rearrange("b (g p j) c -> b g p j c", p=P, j=PACK)
-
         x_sb = []
         for b in range(B):
             xb = xin.tile([P, NT, C], BF16, name="xb", tag="xb")
-            for h in range(2):
-                nc.sync.dma_start(out=xb[:, PACK * h : PACK * h + PACK, :], in_=x_tok[b, h])
+            n = PACK // 2 if b == 0 else PACK
+            for lo in range(0, NT, n):
+                g, j = divmod(lo, PACK)
+                nc.sync.dma_start(out=xb[:, lo : lo + n, :], in_=x_tok[b, g, :, j : j + n, :])
             x_sb.append(xb)
 
-        ident_bf = const.tile([P, P], BF16)
-        make_identity(nc, ident_bf[:])
-        ident_f = const.tile([P, P], F32)
-        make_identity(nc, ident_f[:])
-        offdiag = const.tile([P, P], BF16)
-        nc.vector.tensor_scalar(out=offdiag[:], in0=ident_bf[:], scalar1=-1.0, scalar2=1.0, op0=ALU.mult, op1=ALU.add)
-
-        two_r = const.tile([P, 1], F32)
+        ident = const.tile([P, P], BF16, name="ident")
+        make_identity(nc, ident[:])
+        offdiag = const.tile([P, P], BF16, name="offdiag")
+        nc.vector.tensor_scalar(out=offdiag[:], in0=ident[:], scalar1=-1.0, scalar2=1.0, op0=ALU.mult, op1=ALU.add)
+        ones = const.tile([P, P], BF16, name="ones")
+        nc.vector.memset(ones[:], 1.0)
+        two_r = const.tile([P, 1], F32, name="two_r")
         nc.vector.tensor_scalar(out=two_r[:], in0=r_bf[:], scalar1=2.0, scalar2=None, op0=ALU.mult)
-        m_f = const.tile([P, 1], F32)
+        m_f = const.tile([P, 1], F32, name="m_f")
         nc.vector.tensor_copy(out=m_f[:], in_=m_bf[:])
-        e_m = const.tile([P, 1], F32)
-        nc.scalar.activation(out=e_m[:], in_=m_f[:], func=ACT.Exp)
+        warm = const.tile([P, 1], F32, name="warm")
+        nc.scalar.activation(out=warm[:], in_=ones[:, 0:1], func=ACT.Exp)
+        pieces = []
+        for i in range(2):
+            u = const.tile([P, NT, P], BF16, name="u%d" % i)
+            nc.gpsimd.memset(u[:], 0.0)
+            pieces.append(u)
 
-        state = {}
+        st = {}
 
-        def prep(b):
-            xb = x_sb[b]
-            sq = two.tile([P, NT], F32, name="sq", tag="sq")
-            for a in range(NT):
-                junk = two.tile([P, C], BF16, name="junk", tag="junk")
-                nc.scalar.activation(out=junk[:], in_=xb[:, a, :], func=ACT.Square, accum_out=sq[:, a : a + 1])
-            nhsq = two.tile([P, NT], F32, name="nhsq", tag="nhsq")
-            nc.vector.tensor_scalar(out=nhsq[:], in0=sq[:], scalar1=-0.5, scalar2=None, op0=ALU.mult)
+        def alloc(b):
+            st[b] = {
+                "sq": two.tile([P, NT], F32, name="sq", tag="sq"),
+                "half": two.tile([P, NT], F32, name="half", tag="half"),
+                "rest": two.tile([P, NT], F32, name="rest", tag="rest"),
+                "bias": two.tile([P, NT], F32, name="bias", tag="bias"),
+                "xT": two.tile([P, KC, T], BF16, name="xT", tag="xT"),
+                "rows": two.tile([P, NT, P], BF16, name="rows", tag="rows"),
+                "xg": two.tile([P, NG, C, PACK], BF16, name="xg", tag="xg", align_bytes=64),
+                "xq": two.tile([P, NG, C], U32, name="xq", tag="xq", align_bytes=64),
+                "xs": two.tile([P, NG, C], U8, name="xs", tag="xs", align_bytes=64),
+                "kc": two.tile([P, NT, T], BF16, name="kc", tag="kc"),
+            }
 
-            xT = two.tile([P, KC, T], BF16, name="xT", tag="xT")
-            for a in range(NT):
-                tp = psum_t.tile([P, KC, P], BF16, name="tp", tag="tr")
-                for k in range(KC):
-                    nc.tensor.transpose(tp[:, k, :], xb[:, a, P * k : P * k + P], ident_bf[:])
-                nc.scalar.copy(out=xT[:, :, P * a : P * a + P], in_=tp[:])
-
-            nhsqt = two.tile([P, T], F32, name="nhsqt", tag="nhsqt")
-            for h in range(T // BANK):
-                bc = psum_t.tile([P, BANK], F32, name="bc", tag="tr")
-                for i in range(BANK // P):
-                    a = h * (BANK // P) + i
-                    nc.tensor.transpose(bc[:, P * i : P * i + P], nhsq[:, a : a + 1].to_broadcast([P, P]), ident_f[:])
-                nc.scalar.copy(out=nhsqt[:, BANK * h : BANK * h + BANK], in_=bc[:])
-
-            xg = two.tile([P, NG, C, PACK], BF16, name="xg", tag="xg", align_bytes=64)
-            xq = two.tile([P, NG, C], U32, name="xq", tag="xq", align_bytes=64)
-            xs = two.tile([P, NG, C], U8, name="xs", tag="xs", align_bytes=64)
-            for g in range(NG):
-                nc.vector.tensor_copy(
-                    out=xg[:, g].rearrange("p (c i) j -> p c j i", i=4),
-                    in_=xb[:, PACK * g : PACK * g + PACK, :].rearrange("p j (c i) -> p c j i", i=4),
-                )
-            for g in range(NG):
-                nc.vector.quantize_mx(
-                    out=xq[:, g, :].bitcast(FP8X4),
-                    scales=xs[:, g, :],
-                    in_=xg[:, g].rearrange("p c j -> p (c j)"),
-                )
-            kc = two.tile([P, NT, T], BF16, name="kc", tag="kc")
-            kq = two.tile([P, NT, NG, P], U32, name="kq", tag="kq", align_bytes=64)
-            ks = two.tile([P, NT, NG, P], U8, name="ks", tag="ks", align_bytes=64)
-            state[b] = (nhsq, xT, nhsqt, xq, xs, kc, kq, ks)
-
-        def row(b, a):
-            xb = x_sb[b]
-            nhsq, xT, nhsqt, xq, xs, kc, kq, ks = state[b]
-            lo = P * a
-            z = three.tile([P, T], F32, name="z", tag="z")
-            c0 = lo
-            while c0 < T:
-                w = min(BANK, T - c0)
-                gp = psum_g.tile([P, BANK], F32, name="gp", tag="g")
-                for k in range(KC):
-                    nc.tensor.matmul(
-                        gp[:, :w], lhsT=xT[:, k, lo : lo + P], rhs=xT[:, k, c0 : c0 + w],
-                        start=(k == 0), stop=(k == KC - 1),
-                    )
-                nc.vector.scalar_tensor_tensor(
-                    out=z[:, c0 : c0 + w], in0=gp[:, :w], scalar=nhsq[:, a : a + 1], in1=nhsqt[:, c0 : c0 + w],
-                    op0=ALU.add, op1=ALU.add,
-                )
-                c0 += w
-            nc.scalar.activation(out=kc[:, a, lo:T], in_=z[:, lo:T], func=ACT.Exp, bias=m_f[:], scale=two_r[:])
-            nc.vector.tensor_tensor(out=kc[:, a, lo : lo + P], in0=kc[:, a, lo : lo + P], in1=offdiag[:], op=ALU.mult)
-            if a < PACK:
-                nc.vector.tensor_scalar(
-                    out=kc[:, a, BANK:T], in0=kc[:, a, BANK:T], scalar1=e_m[:], scalar2=None, op0=ALU.min
-                )
-            kt = None
-            if a < NT - 1:
-                kt = psum_t.tile([P, NT, P], BF16, name="kt", tag="tr")
-                for s in range(a + 1, NT):
-                    nc.tensor.transpose(kt[:, s, :], kc[:, a, P * s : P * s + P], ident_bf[:])
-            grp = four.tile([P, NG, P, PACK], BF16, name="grp", tag="grp", align_bytes=64)
-            for g in range(NG):
-                nd = max(0, min(PACK, a - PACK * g + 1))
-                if nd > 0:
-                    nc.vector.tensor_scalar(
-                        out=grp[:, g, :, 0:nd],
-                        in0=kc[:, PACK * g : PACK * g + nd, lo : lo + P].rearrange("p j t -> p t j"),
-                        scalar1=e_m[:], scalar2=None, op0=ALU.min,
-                    )
-                if nd == 0:
-                    nc.scalar.copy(out=grp[:, g], in_=kt[:, PACK * g : PACK * g + PACK, :].rearrange("p j t -> p t j"))
-                elif nd < PACK:
-                    nc.vector.tensor_scalar(
-                        out=grp[:, g, :, nd:PACK],
-                        in0=kt[:, PACK * g + nd : PACK * g + PACK, :].rearrange("p j t -> p t j"),
-                        scalar1=e_m[:], scalar2=None, op0=ALU.min,
-                    )
-            nc.vector.quantize_mx(
-                out=kq[:, a].rearrange("p g t -> p (g t)").bitcast(FP8X4),
-                scales=ks[:, a].rearrange("p g t -> p (g t)"),
-                in_=grp[:].rearrange("p g t j -> p (g t j)"),
+        def square_s(b, a):
+            junk = two.tile([P, C], BF16, name="junk", tag="junk")
+            nc.scalar.activation(
+                out=junk[:], in_=x_sb[b][:, a, :], func=ACT.Square, accum_out=st[b]["sq"][:, a : a + 1]
             )
+
+        def square_v(b, a):
+            junk = two.tile([P, C], F32, name="junkv", tag="junkv")
+            nc.vector.scalar_tensor_tensor(
+                out=junk[:], in0=x_sb[b][:, a, :], scalar=1.0, in1=x_sb[b][:, a, :],
+                op0=ALU.mult, op1=ALU.mult, accum_out=st[b]["sq"][:, a : a + 1],
+            )
+
+        def x_transpose(b, a, copy):
+            tp = psum_w.tile([P, KC, P], BF16, name="tp", tag="w")
+            for k in range(KC):
+                nc.tensor.transpose(tp[:, k, :], x_sb[b][:, a, P * k : P * k + P], ident[:])
+            copy(out=st[b]["xT"][:, :, P * a : P * a + P], in_=tp[:])
+
+        def norms(b, eng):
+            d, u = st[b], pieces[b % 2]
+            eng.tensor_scalar(out=d["half"][:], in0=d["sq"][:], scalar1=-0.5, scalar2=None, op0=ALU.mult)
+            eng.tensor_copy(out=u[:, :, 0], in_=d["half"][:])
+            eng.tensor_tensor(out=d["rest"][:], in0=d["half"][:], in1=u[:, :, 0], op=ALU.subtract)
+            eng.tensor_copy(out=u[:, :, 1], in_=d["rest"][:])
+            eng.tensor_tensor(out=u[:, :, 2], in0=d["rest"][:], in1=u[:, :, 1], op=ALU.subtract)
+            eng.tensor_scalar(
+                out=d["bias"][:], in0=d["half"][:], scalar1=two_r[:], scalar2=m_f[:], op0=ALU.mult, op1=ALU.add
+            )
+
+        def norm_rows(b):
+            tp = psum_w.tile([P, NT, P], BF16, name="tpr", tag="w")
+            for a in range(NT):
+                nc.tensor.transpose(tp[:, a, :], pieces[b % 2][:, a, :], ident[:])
+            nc.scalar.copy(out=st[b]["rows"][:], in_=tp[:])
+
+        def x_regroup(b, g):
+            nc.vector.tensor_copy(
+                out=st[b]["xg"][:, g].rearrange("p (c i) j -> p c j i", i=4),
+                in_=x_sb[b][:, PACK * g : PACK * g + PACK, :].rearrange("p j (c i) -> p c j i", i=4),
+            )
+
+        def x_quantize(b, g):
+            d = st[b]
+            nc.vector.quantize_mx(
+                out=d["xq"][:, g, :].bitcast(FP8X4),
+                scales=d["xs"][:, g, :],
+                in_=d["xg"][:, g].rearrange("p c j -> p (c j)"),
+            )
+
+        gp_of = {}
+
+        def gram_open(b, a, c0):
+            w = min(BANK, T - c0)
+            gp = psum_w.tile([P, BANK], F32, name="gp", tag="w")
+            gp_of[b, a, c0] = gp
+            xT = st[b]["xT"]
+            for k in range(KC):
+                nc.tensor.matmul(
+                    gp[:, :w], lhsT=xT[:, k, P * a : P * a + P], rhs=xT[:, k, c0 : c0 + w], start=(k == 0), stop=False
+                )
+
+        def gram_close(b, a, c0):
+            w = min(BANK, T - c0)
+            gp = gp_of[b, a, c0]
+            d = st[b]
+            nc.tensor.matmul(
+                gp[:, :w], lhsT=ones[:], rhs=d["rows"][:].rearrange("p a t -> p (a t)")[:, c0 : c0 + w],
+                start=False, stop=True,
+            )
+            nc.scalar.activation(
+                out=d["kc"][:, a, c0 : c0 + w], in_=gp[:, :w], func=ACT.Exp, bias=d["bias"][:, a : a + 1], scale=two_r[:]
+            )
+
+        def mask(b, a):
+            blk = st[b]["kc"][:, a, P * a : P * a + P]
+            nc.vector.tensor_tensor(out=blk, in0=blk, in1=offdiag[:], op=ALU.mult)
+
+        grp_of, codes_of, op_of = {}, {}, {}
+
+        def mirror(b, a):
+            kc, lo = st[b]["kc"], P * a
+            grp = four.tile([P, NG, P, PACK], BF16, name="grp", tag="grp", align_bytes=64)
+            grp_of[b, a] = grp
+            if a == NT - 1:
+                return
+            kt = psum_w.tile([P, NT, P], BF16, name="kt", tag="w")
+            for s in range(a + 1, NT):
+                nc.tensor.transpose(kt[:, s, :], kc[:, a, P * s : P * s + P], ident[:])
+            end = PACK * (a // PACK) + PACK
+            if a + 1 < end:
+                nc.scalar.copy(out=kc[:, a + 1 : end, lo : lo + P], in_=kt[:, a + 1 : end, :])
+            if end < NT:
+                nc.scalar.copy(out=grp[:, 1], in_=kt[:, end:NT, :].rearrange("p j t -> p t j"))
+
+        def regroup(b, a):
+            kc, lo, grp = st[b]["kc"], P * a, grp_of[b, a]
+            for g in range(a // PACK + 1):
+                nc.vector.tensor_copy(
+                    out=grp[:, g], in_=kc[:, PACK * g : PACK * g + PACK, lo : lo + P].rearrange("p j t -> p t j")
+                )
+
+        def k_quantize(b, a):
+            kq = four.tile([P, NG, P], U32, name="kq", tag="kq", align_bytes=64)
+            ks = four.tile([P, NG, P], U8, name="ks", tag="ks", align_bytes=64)
+            codes_of[b, a] = (kq, ks)
+            nc.vector.quantize_mx(
+                out=kq[:].rearrange("p g t -> p (g t)").bitcast(FP8X4),
+                scales=ks[:].rearrange("p g t -> p (g t)"),
+                in_=grp_of[b, a][:].rearrange("p g t j -> p (g t j)"),
+            )
+
+        def multiply(b, a):
+            d = st[b]
+            kq, ks = codes_of[b, a]
             op = psum_o.tile([P, C], F32, name="op", tag="o")
+            op_of[b, a] = op
             for g in range(NG):
                 nc.tensor.matmul_mx(
                     out=op[:],
-                    lhsT=kq[:, a, g, :].bitcast(FP8X4), lhsT_scale=ks[:, a, g, :],
-                    rhs=xq[:, g, :].bitcast(FP8X4), rhs_scale=xs[:, g, :],
+                    lhsT=kq[:, g, :].bitcast(FP8X4), lhsT_scale=ks[:, g, :],
+                    rhs=d["xq"][:, g, :].bitcast(FP8X4), rhs_scale=d["xs"][:, g, :],
                     start=(g == 0), stop=(g == NG - 1),
                 )
+
+        def finish(b, a):
             res = four.tile([P, C], F32, name="res", tag="res")
-            nc.vector.tensor_tensor(out=res[:], in0=op[:], in1=xb[:, a, :], op=ALU.add)
+            nc.vector.tensor_tensor(out=res[:], in0=op_of[b, a][:], in1=x_sb[b][:, a, :], op=ALU.add)
             nc.sync.dma_start(out=out_tok[b, a // PACK, :, a % PACK, :], in_=res[:])
 
-        prep(0)
-        for b in range(B):
+        rows = [(b, a) for b in range(B) for a in range(NT)]
+        banks = [(b, a, c0) for b, a in rows for c0 in range(P * a, T, BANK)]
+        last_bank = {}
+        for i, (b, a, c0) in enumerate(banks):
+            last_bank[b, a] = i + 1
+
+        with ExitStack() as pinned:
+            pinned.enter_context(tc.manual_schedule())
+            alloc(0)
             for a in range(NT):
-                row(b, a)
-                if a == 2 and b + 1 < B:
-                    prep(b + 1)
+                x_transpose(0, a, nc.scalar.copy if a % 2 else nc.vector.tensor_copy)
+                if a % 2:
+                    square_s(0, a)
+                else:
+                    square_v(0, a)
+            for bank in banks[:HEAD]:
+                gram_open(*bank)
+            norms(0, nc.vector)
+            norm_rows(0)
+            for bank in banks[:HEAD]:
+                gram_close(*bank)
+            for g in range(NG):
+                x_regroup(0, g)
+                x_quantize(0, g)
+            mask(0, 0)
+            done = [HEAD]
+
+            def next_bank(row):
+                if done[0] < min(len(banks), last_bank[row] + LEAD):
+                    gram_open(*banks[done[0]])
+                    gram_close(*banks[done[0]])
+                    done[0] += 1
+
+            n = len(rows)
+            for i in range(-1, n + 1):
+                cur = rows[i] if 0 <= i < n else None
+                nxt = rows[i + 1] if i + 1 < n else None
+                tgt = nxt if nxt else rows[-1]
+                prep = cur[0] + 1 if cur and cur[0] + 1 < B else None
+                if prep and cur[1] == 0:
+                    alloc(prep)
+                next_bank(tgt)
+                if nxt:
+                    mirror(*nxt)
+                if prep and 1 <= cur[1] <= 4:
+                    x_transpose(prep, 2 * cur[1] - 2, nc.scalar.copy)
+                    x_transpose(prep, 2 * cur[1] - 1, nc.scalar.copy)
+                if prep and cur[1] == 4:
+                    norm_rows(prep)
+                if nxt:
+                    regroup(*nxt)
+                if i + 2 < n:
+                    mask(*rows[i + 2])
+                next_bank(tgt)
+                if i >= 1:
+                    finish(*rows[i - 1])
+                if nxt:
+                    k_quantize(*nxt)
+                if cur:
+                    multiply(*cur)
+                next_bank(tgt)
+                if prep:
+                    if cur[1] < 4:
+                        square_s(prep, 2 * cur[1])
+                        square_s(prep, 2 * cur[1] + 1)
+                    if cur[1] == 3:
+                        norms(prep, nc.gpsimd)
+                    if cur[1] in (4, 6):
+                        x_regroup(prep, (cur[1] - 4) // 2)
+                    if cur[1] in (5, 7):
+                        x_quantize(prep, (cur[1] - 5) // 2)

@@ -10,6 +10,7 @@ U8 = mybir.dt.uint8
 FP8X4 = mybir.dt.float8_e4m3fn_x4
 ALU = mybir.AluOpType
 ACT = mybir.ActivationFunctionType
+AX = mybir.AxisListType
 
 B, T, C = 4, 1024, 512
 P = 128
@@ -52,6 +53,8 @@ def tile_k_attention_ex_t_kernel(tc, x, r_sigma, margin, out):
 
         ident = const.tile([P, P], BF16, name="ident")
         make_identity(nc, ident[:])
+        ident_f = const.tile([P, P], F32, name="ident_f")
+        make_identity(nc, ident_f[:])
         offdiag = const.tile([P, P], BF16, name="offdiag")
         nc.vector.tensor_scalar(out=offdiag[:], in0=ident[:], scalar1=-1.0, scalar2=1.0, op0=ALU.mult, op1=ALU.add)
         ones = const.tile([P, P], BF16, name="ones")
@@ -64,9 +67,15 @@ def tile_k_attention_ex_t_kernel(tc, x, r_sigma, margin, out):
         nc.scalar.activation(out=warm[:], in_=ones[:, 0:1], func=ACT.Exp)
         pieces = []
         for i in range(2):
-            u = const.tile([P, NT, P], BF16, name="u%d" % i)
+            u = const.tile([P, P], BF16, name="u%d" % i)
             nc.gpsimd.memset(u[:], 0.0)
             pieces.append(u)
+        rowsum = const.tile([P, NT], F32, name="rowsum")
+        nc.vector.tensor_reduce(
+            out=rowsum[:], in_=ident[:, 0 : 3 * NT].rearrange("p (a i) -> p a i", i=3), axis=AX.X, op=ALU.add
+        )
+        pick = const.tile([P, NT, P], BF16, name="pick")
+        nc.vector.tensor_copy(out=pick[:], in_=rowsum[:].unsqueeze(2).to_broadcast([P, NT, P]))
 
         st = {}
 
@@ -77,7 +86,7 @@ def tile_k_attention_ex_t_kernel(tc, x, r_sigma, margin, out):
                 "rest": two.tile([P, NT], F32, name="rest", tag="rest"),
                 "bias": two.tile([P, NT], F32, name="bias", tag="bias"),
                 "xT": two.tile([P, KC, T], BF16, name="xT", tag="xT"),
-                "rows": two.tile([P, NT, P], BF16, name="rows", tag="rows"),
+                "rows": two.tile([P, P], BF16, name="rows", tag="rows"),
                 "xg": two.tile([P, NG, C, PACK], BF16, name="xg", tag="xg", align_bytes=64),
                 "xq": two.tile([P, NG, C], U32, name="xq", tag="xq", align_bytes=64),
                 "xs": two.tile([P, NG, C], U8, name="xs", tag="xs", align_bytes=64),
@@ -98,13 +107,18 @@ def tile_k_attention_ex_t_kernel(tc, x, r_sigma, margin, out):
             )
 
         def x_transpose(b, a, copy):
-            tp = psum_w.tile([P, KC, P], BF16, name="tp", tag="w")
-            for k in range(KC):
-                nc.tensor.transpose(tp[:, k, :], x_sb[b][:, a, P * k : P * k + P], ident[:])
-            copy(out=st[b]["xT"][:, :, P * a : P * a + P], in_=tp[:])
+            tp = psum_w.tile([P, KC // 2, P], F32, name="tp", tag="w")
+            words = x_sb[b][:, a, :].bitcast(F32)
+            for h in range(KC // 2):
+                nc.tensor.transpose(tp[:, h, :], words[:, P * h : P * h + P], ident_f[:])
+            copy(
+                out=st[b]["xT"][:].rearrange("p (h e) t -> p h e t", e=2)[:, :, :, P * a : P * a + P],
+                in_=tp[:].bitcast(BF16).rearrange("p h (t e) -> p h e t", e=2),
+            )
 
         def norms(b, eng):
-            d, u = st[b], pieces[b % 2]
+            d = st[b]
+            u = pieces[b % 2][:, 0 : 3 * NT].rearrange("p (a i) -> p a i", i=3)
             eng.tensor_scalar(out=d["half"][:], in0=d["sq"][:], scalar1=-0.5, scalar2=None, op0=ALU.mult)
             eng.tensor_copy(out=u[:, :, 0], in_=d["half"][:])
             eng.tensor_tensor(out=d["rest"][:], in0=d["half"][:], in1=u[:, :, 0], op=ALU.subtract)
@@ -115,9 +129,8 @@ def tile_k_attention_ex_t_kernel(tc, x, r_sigma, margin, out):
             )
 
         def norm_rows(b):
-            tp = psum_w.tile([P, NT, P], BF16, name="tpr", tag="w")
-            for a in range(NT):
-                nc.tensor.transpose(tp[:, a, :], pieces[b % 2][:, a, :], ident[:])
+            tp = psum_w.tile([P, P], BF16, name="tpr", tag="w")
+            nc.tensor.transpose(tp[:], pieces[b % 2][:], ident[:])
             nc.scalar.copy(out=st[b]["rows"][:], in_=tp[:])
 
         def x_regroup(b, g):
@@ -150,10 +163,11 @@ def tile_k_attention_ex_t_kernel(tc, x, r_sigma, margin, out):
             w = min(BANK, T - c0)
             gp = gp_of[b, a, c0]
             d = st[b]
-            nc.tensor.matmul(
-                gp[:, :w], lhsT=ones[:], rhs=d["rows"][:].rearrange("p a t -> p (a t)")[:, c0 : c0 + w],
-                start=False, stop=True,
-            )
+            for i in range(w // P):
+                nc.tensor.matmul(
+                    gp[:, P * i : P * i + P], lhsT=pick[:, c0 // P + i, :], rhs=d["rows"][:],
+                    start=False, stop=(i == w // P - 1),
+                )
             nc.scalar.activation(
                 out=d["kc"][:, a, c0 : c0 + w], in_=gp[:, :w], func=ACT.Exp, bias=d["bias"][:, a : a + 1], scale=two_r[:]
             )
@@ -258,6 +272,8 @@ def tile_k_attention_ex_t_kernel(tc, x, r_sigma, margin, out):
                 next_bank(tgt)
                 if nxt:
                     mirror(*nxt)
+                if prep and cur[1] == 3:
+                    norms(prep, nc.gpsimd)
                 if prep and 1 <= cur[1] <= 4:
                     x_transpose(prep, 2 * cur[1] - 2, nc.scalar.copy)
                     x_transpose(prep, 2 * cur[1] - 1, nc.scalar.copy)
@@ -276,12 +292,13 @@ def tile_k_attention_ex_t_kernel(tc, x, r_sigma, margin, out):
                     multiply(*cur)
                 next_bank(tgt)
                 if prep:
-                    if cur[1] < 4:
-                        square_s(prep, 2 * cur[1])
-                        square_s(prep, 2 * cur[1] + 1)
-                    if cur[1] == 3:
-                        norms(prep, nc.gpsimd)
+                    if cur[1] < 2:
+                        for a in range(4 * cur[1], 4 * cur[1] + 4):
+                            if a % 2:
+                                square_s(prep, a)
+                            else:
+                                square_v(prep, a)
+                    if cur[1] in (1, 3):
+                        x_regroup(prep, cur[1] // 2)
                     if cur[1] in (4, 6):
-                        x_regroup(prep, (cur[1] - 4) // 2)
-                    if cur[1] in (5, 7):
-                        x_quantize(prep, (cur[1] - 5) // 2)
+                        x_quantize(prep, cur[1] // 2 - 2)

@@ -19,8 +19,11 @@ KC = C // P
 PACK = 4
 NG = T // (P * PACK)
 BANK = 512
-LEAD = 2
-HEAD = 3
+LEAD = 3
+HEAD = 4
+
+WARM = 6
+V_SQUARES = 5
 
 FLOPS = 2 * (2 * B * T * T * C)
 
@@ -31,6 +34,7 @@ def tile_k_attention_ex_t_kernel(tc, x, r_sigma, margin, out):
         const = ctx.enter_context(tc.tile_pool(name="const", bufs=1))
         xin = ctx.enter_context(tc.tile_pool(name="xin", bufs=B))
         two = ctx.enter_context(tc.tile_pool(name="two", bufs=2))
+        eight = ctx.enter_context(tc.tile_pool(name="eight", bufs=8))
         four = ctx.enter_context(tc.tile_pool(name="four", bufs=4))
         psum_w = ctx.enter_context(tc.psum_pool(name="psum_w", bufs=6))
         psum_o = ctx.enter_context(tc.psum_pool(name="psum_o", bufs=2))
@@ -51,6 +55,8 @@ def tile_k_attention_ex_t_kernel(tc, x, r_sigma, margin, out):
                 nc.sync.dma_start(out=xb[:, lo : lo + n, :], in_=x_tok[b, g, :, j : j + n, :])
             x_sb.append(xb)
 
+        zeros = const.tile([P, BANK], BF16, name="zeros")
+        nc.vector.memset(zeros[:], 0.0)
         ident = const.tile([P, P], BF16, name="ident")
         make_identity(nc, ident[:])
         ident_f = const.tile([P, P], F32, name="ident_f")
@@ -178,10 +184,13 @@ def tile_k_attention_ex_t_kernel(tc, x, r_sigma, margin, out):
 
         grp_of, codes_of, op_of = {}, {}, {}
 
+        def group(b, a):
+            if (b, a) not in grp_of:
+                grp_of[b, a] = eight.tile([P, NG, P, PACK], BF16, name="grp", tag="grp", align_bytes=64)
+            return grp_of[b, a]
+
         def mirror(b, a):
             kc, lo = st[b]["kc"], P * a
-            grp = four.tile([P, NG, P, PACK], BF16, name="grp", tag="grp", align_bytes=64)
-            grp_of[b, a] = grp
             if a == NT - 1:
                 return
             kt = psum_w.tile([P, NT, P], BF16, name="kt", tag="w")
@@ -191,14 +200,13 @@ def tile_k_attention_ex_t_kernel(tc, x, r_sigma, margin, out):
             if a + 1 < end:
                 nc.scalar.copy(out=kc[:, a + 1 : end, lo : lo + P], in_=kt[:, a + 1 : end, :])
             if end < NT:
-                nc.scalar.copy(out=grp[:, 1], in_=kt[:, end:NT, :].rearrange("p j t -> p t j"))
+                nc.scalar.copy(out=group(b, a)[:, 1], in_=kt[:, end:NT, :].rearrange("p j t -> p t j"))
 
-        def regroup(b, a):
-            kc, lo, grp = st[b]["kc"], P * a, grp_of[b, a]
-            for g in range(a // PACK + 1):
-                nc.vector.tensor_copy(
-                    out=grp[:, g], in_=kc[:, PACK * g : PACK * g + PACK, lo : lo + P].rearrange("p j t -> p t j")
-                )
+        def regroup(b, a, g, copy):
+            copy(
+                out=group(b, a)[:, g],
+                in_=st[b]["kc"][:, PACK * g : PACK * g + PACK, P * a : P * a + P].rearrange("p j t -> p t j"),
+            )
 
         def k_quantize(b, a):
             kq = four.tile([P, NG, P], U32, name="kq", tag="kq", align_bytes=64)
@@ -237,8 +245,12 @@ def tile_k_attention_ex_t_kernel(tc, x, r_sigma, margin, out):
         with ExitStack() as pinned:
             pinned.enter_context(tc.manual_schedule())
             alloc(0)
+            for i in range(WARM):
+                wp = psum_w.tile([P, BANK], F32, name="wp", tag="w")
+                nc.tensor.matmul(wp[:], lhsT=zeros[:, 0:P], rhs=zeros[:], start=True, stop=True)
             for a in range(NT):
                 x_transpose(0, a, nc.scalar.copy if a % 2 else nc.vector.tensor_copy)
+            for a in range(NT):
                 if a % 2:
                     square_s(0, a)
                 else:
@@ -269,36 +281,45 @@ def tile_k_attention_ex_t_kernel(tc, x, r_sigma, margin, out):
                 prep = cur[0] + 1 if cur and cur[0] + 1 < B else None
                 if prep and cur[1] == 0:
                     alloc(prep)
+                if prep and cur[1] == 1:
+                    norms(prep, nc.gpsimd)
+                next_bank(tgt)
+                if nxt and nxt < (B - 1, NT - 2):
+                    mirror(*nxt)
+                if nxt == (B - 1, NT - 3):
+                    mirror(B - 1, NT - 2)
+                if prep and cur[1] < 4:
+                    x_transpose(prep, 2 * cur[1], nc.scalar.copy)
+                    x_transpose(prep, 2 * cur[1] + 1, nc.scalar.copy)
+                if prep and cur[1] == 3:
+                    norm_rows(prep)
                 next_bank(tgt)
                 if nxt:
-                    mirror(*nxt)
-                if prep and cur[1] == 3:
-                    norms(prep, nc.gpsimd)
-                if prep and 1 <= cur[1] <= 4:
-                    x_transpose(prep, 2 * cur[1] - 2, nc.scalar.copy)
-                    x_transpose(prep, 2 * cur[1] - 1, nc.scalar.copy)
-                if prep and cur[1] == 4:
-                    norm_rows(prep)
-                if nxt:
-                    regroup(*nxt)
+                    b, a = nxt
+                    if b < B - 1:
+                        for g in range(a // PACK + 1):
+                            regroup(b, a, g, nc.vector.tensor_copy)
+                    else:
+                        regroup(b, a, a // PACK, nc.scalar.copy if a > 5 else nc.vector.tensor_copy)
+                        if a in (4, 5):
+                            regroup(b, 2 * a - 4, 0, nc.scalar.copy)
+                            regroup(b, 2 * a - 3, 0, nc.scalar.copy)
                 if i + 2 < n:
                     mask(*rows[i + 2])
-                next_bank(tgt)
                 if i >= 1:
                     finish(*rows[i - 1])
                 if nxt:
                     k_quantize(*nxt)
                 if cur:
                     multiply(*cur)
+                if prep and cur[1] == 0:
+                    for a in range(NT):
+                        if a < V_SQUARES:
+                            square_v(prep, a)
+                        else:
+                            square_s(prep, a)
+                if prep and cur[1] in (1, 2):
+                    x_regroup(prep, cur[1] - 1)
+                if prep and cur[1] in (6, 7):
+                    x_quantize(prep, cur[1] - 6)
                 next_bank(tgt)
-                if prep:
-                    if cur[1] < 2:
-                        for a in range(4 * cur[1], 4 * cur[1] + 4):
-                            if a % 2:
-                                square_s(prep, a)
-                            else:
-                                square_v(prep, a)
-                    if cur[1] in (1, 3):
-                        x_regroup(prep, cur[1] // 2)
-                    if cur[1] in (4, 6):
-                        x_quantize(prep, cur[1] // 2 - 2)

@@ -74,7 +74,7 @@ def tile_k_attention_ex_t_kernel(tc, x, r_sigma, margin, out):
         pieces = []
         for i in range(2):
             u = const.tile([P, P], BF16, name="u%d" % i)
-            nc.gpsimd.memset(u[:], 0.0)
+            nc.vector.memset(u[:], 0.0)
             pieces.append(u)
         rowsum = const.tile([P, NT], F32, name="rowsum")
         nc.vector.tensor_reduce(
@@ -122,17 +122,24 @@ def tile_k_attention_ex_t_kernel(tc, x, r_sigma, margin, out):
                 in_=tp[:].bitcast(BF16).rearrange("p h (t e) -> p h e t", e=2),
             )
 
-        def norms(b, eng):
+        def norm_step(b, i):
             d = st[b]
             u = pieces[b % 2][:, 0 : 3 * NT].rearrange("p (a i) -> p a i", i=3)
-            eng.tensor_scalar(out=d["half"][:], in0=d["sq"][:], scalar1=-0.5, scalar2=None, op0=ALU.mult)
-            eng.tensor_copy(out=u[:, :, 0], in_=d["half"][:])
-            eng.tensor_tensor(out=d["rest"][:], in0=d["half"][:], in1=u[:, :, 0], op=ALU.subtract)
-            eng.tensor_copy(out=u[:, :, 1], in_=d["rest"][:])
-            eng.tensor_tensor(out=u[:, :, 2], in0=d["rest"][:], in1=u[:, :, 1], op=ALU.subtract)
-            eng.tensor_scalar(
-                out=d["bias"][:], in0=d["half"][:], scalar1=two_r[:], scalar2=m_f[:], op0=ALU.mult, op1=ALU.add
-            )
+            half, rest = d["half"][:], d["rest"][:]
+            if i == 0:
+                nc.vector.tensor_scalar(out=half, in0=d["sq"][:], scalar1=-0.5, scalar2=None, op0=ALU.mult)
+            elif i == 1:
+                nc.vector.tensor_copy(out=u[:, :, 0], in_=half)
+            elif i == 2:
+                nc.vector.tensor_tensor(out=rest, in0=half, in1=u[:, :, 0], op=ALU.subtract)
+            elif i == 3:
+                nc.vector.tensor_copy(out=u[:, :, 1], in_=rest)
+            elif i == 4:
+                nc.vector.tensor_tensor(out=u[:, :, 2], in0=rest, in1=u[:, :, 1], op=ALU.subtract)
+            else:
+                nc.vector.tensor_scalar(
+                    out=d["bias"][:], in0=half, scalar1=two_r[:], scalar2=m_f[:], op0=ALU.mult, op1=ALU.add
+                )
 
         def norm_rows(b):
             tp = psum_w.tile([P, P], BF16, name="tpr", tag="w")
@@ -257,7 +264,8 @@ def tile_k_attention_ex_t_kernel(tc, x, r_sigma, margin, out):
                     square_v(0, a)
             for bank in banks[:HEAD]:
                 gram_open(*bank)
-            norms(0, nc.vector)
+            for i in range(6):
+                norm_step(0, i)
             norm_rows(0)
             for bank in banks[:HEAD]:
                 gram_close(*bank)
@@ -281,8 +289,7 @@ def tile_k_attention_ex_t_kernel(tc, x, r_sigma, margin, out):
                 prep = cur[0] + 1 if cur and cur[0] + 1 < B else None
                 if prep and cur[1] == 0:
                     alloc(prep)
-                if prep and cur[1] == 1:
-                    norms(prep, nc.gpsimd)
+                spread = prep and cur[1] in (1, 2)
                 next_bank(tgt)
                 if nxt and nxt < (B - 1, NT - 2):
                     mirror(*nxt)
@@ -304,12 +311,18 @@ def tile_k_attention_ex_t_kernel(tc, x, r_sigma, margin, out):
                         if a in (4, 5):
                             regroup(b, 2 * a - 4, 0, nc.scalar.copy)
                             regroup(b, 2 * a - 3, 0, nc.scalar.copy)
+                if spread:
+                    norm_step(prep, 3 * cur[1] - 3)
                 if i + 2 < n:
                     mask(*rows[i + 2])
                 if i >= 1:
                     finish(*rows[i - 1])
+                if spread:
+                    norm_step(prep, 3 * cur[1] - 2)
                 if nxt:
                     k_quantize(*nxt)
+                if spread:
+                    norm_step(prep, 3 * cur[1] - 1)
                 if cur:
                     multiply(*cur)
                 if prep and cur[1] == 0:

@@ -83,11 +83,14 @@ def tile_k_attention_ex_t_kernel(tc, x, r_sigma, margin, out):
         pick = const.tile([P, NT, P], BF16, name="pick")
         nc.vector.tensor_copy(out=pick[:], in_=rowsum[:].unsqueeze(2).to_broadcast([P, NT, P]))
 
+        sq_of = []
+        for b in range(B):
+            sq = const.tile([P, NT], F32, name="sq%d" % b)
+            sq_of.append(sq)
         st = {}
 
         def alloc(b):
             st[b] = {
-                "sq": two.tile([P, NT], F32, name="sq", tag="sq"),
                 "half": two.tile([P, NT], F32, name="half", tag="half"),
                 "rest": two.tile([P, NT], F32, name="rest", tag="rest"),
                 "bias": two.tile([P, NT], F32, name="bias", tag="bias"),
@@ -102,32 +105,44 @@ def tile_k_attention_ex_t_kernel(tc, x, r_sigma, margin, out):
         def square_s(b, a):
             junk = two.tile([P, C], BF16, name="junk", tag="junk")
             nc.scalar.activation(
-                out=junk[:], in_=x_sb[b][:, a, :], func=ACT.Square, accum_out=st[b]["sq"][:, a : a + 1]
+                out=junk[:], in_=x_sb[b][:, a, :], func=ACT.Square, accum_out=sq_of[b][:, a : a + 1]
             )
 
         def square_v(b, a):
             junk = two.tile([P, C], F32, name="junkv", tag="junkv")
             nc.vector.scalar_tensor_tensor(
                 out=junk[:], in0=x_sb[b][:, a, :], scalar=1.0, in1=x_sb[b][:, a, :],
-                op0=ALU.mult, op1=ALU.mult, accum_out=st[b]["sq"][:, a : a + 1],
+                op0=ALU.mult, op1=ALU.mult, accum_out=sq_of[b][:, a : a + 1],
             )
 
-        def x_transpose(b, a, copy):
-            tp = psum_w.tile([P, KC // 2, P], F32, name="tp", tag="w")
+        def x_ops(b, a, copy):
             words = x_sb[b][:, a, :].bitcast(F32)
-            for h in range(KC // 2):
+            box = []
+
+            def one(h):
+                if h == 0:
+                    tp = psum_w.tile([P, KC // 2, P], F32, name="tp", tag="w")
+                    box.append(tp)
+                tp = box[0]
                 nc.tensor.transpose(tp[:, h, :], words[:, P * h : P * h + P], ident_f[:])
-            copy(
-                out=st[b]["xT"][:].rearrange("p (h e) t -> p h e t", e=2)[:, :, :, P * a : P * a + P],
-                in_=tp[:].bitcast(BF16).rearrange("p h (t e) -> p h e t", e=2),
-            )
+                if h == KC // 2 - 1:
+                    copy(
+                        out=st[b]["xT"][:].rearrange("p (h e) t -> p h e t", e=2)[:, :, :, P * a : P * a + P],
+                        in_=tp[:].bitcast(BF16).rearrange("p h (t e) -> p h e t", e=2),
+                    )
+
+            return [(one, h) for h in range(KC // 2)]
+
+        def run(ops):
+            for f, q in ops:
+                f(q)
 
         def norm_step(b, i):
             d = st[b]
             u = pieces[b % 2][:, 0 : 3 * NT].rearrange("p (a i) -> p a i", i=3)
             half, rest = d["half"][:], d["rest"][:]
             if i == 0:
-                nc.vector.tensor_scalar(out=half, in0=d["sq"][:], scalar1=-0.5, scalar2=None, op0=ALU.mult)
+                nc.vector.tensor_scalar(out=half, in0=sq_of[b][:], scalar1=-0.5, scalar2=None, op0=ALU.mult)
             elif i == 1:
                 nc.vector.tensor_copy(out=u[:, :, 0], in_=half)
             elif i == 2:
@@ -141,10 +156,13 @@ def tile_k_attention_ex_t_kernel(tc, x, r_sigma, margin, out):
                     out=d["bias"][:], in0=half, scalar1=two_r[:], scalar2=m_f[:], op0=ALU.mult, op1=ALU.add
                 )
 
-        def norm_rows(b):
-            tp = psum_w.tile([P, P], BF16, name="tpr", tag="w")
-            nc.tensor.transpose(tp[:], pieces[b % 2][:], ident[:])
-            nc.scalar.copy(out=st[b]["rows"][:], in_=tp[:])
+        def norm_ops(b):
+            def one(q):
+                tp = psum_w.tile([P, P], BF16, name="tpr", tag="w")
+                nc.tensor.transpose(tp[:], pieces[b % 2][:], ident[:])
+                nc.scalar.copy(out=st[b]["rows"][:], in_=tp[:])
+
+            return [(one, 0)]
 
         def x_regroup(b, g):
             nc.vector.tensor_copy(
@@ -162,28 +180,34 @@ def tile_k_attention_ex_t_kernel(tc, x, r_sigma, margin, out):
 
         gp_of = {}
 
-        def gram_open(b, a, c0):
+        def gram_ops(b, a, c0):
             w = min(BANK, T - c0)
-            gp = psum_w.tile([P, BANK], F32, name="gp", tag="w")
-            gp_of[b, a, c0] = gp
             xT = st[b]["xT"]
-            for k in range(KC):
+            box = []
+
+            def chunk(k):
+                if k == 0:
+                    gp = psum_w.tile([P, BANK], F32, name="gp", tag="w")
+                    box.append(gp)
+                gp = box[0]
                 nc.tensor.matmul(
                     gp[:, :w], lhsT=xT[:, k, P * a : P * a + P], rhs=xT[:, k, c0 : c0 + w], start=(k == 0), stop=False
                 )
 
-        def gram_close(b, a, c0):
-            w = min(BANK, T - c0)
-            gp = gp_of[b, a, c0]
-            d = st[b]
-            for i in range(w // P):
+            def norm(i):
+                d = st[b]
+                gp = box[0]
+                last = i == w // P - 1
                 nc.tensor.matmul(
-                    gp[:, P * i : P * i + P], lhsT=pick[:, c0 // P + i, :], rhs=d["rows"][:],
-                    start=False, stop=(i == w // P - 1),
+                    gp[:, P * i : P * i + P], lhsT=pick[:, c0 // P + i, :], rhs=d["rows"][:], start=False, stop=last
                 )
-            nc.scalar.activation(
-                out=d["kc"][:, a, c0 : c0 + w], in_=gp[:, :w], func=ACT.Exp, bias=d["bias"][:, a : a + 1], scale=two_r[:]
-            )
+                if last:
+                    nc.scalar.activation(
+                        out=d["kc"][:, a, c0 : c0 + w], in_=gp[:, :w], func=ACT.Exp,
+                        bias=d["bias"][:, a : a + 1], scale=two_r[:],
+                    )
+
+            return [(chunk, k) for k in range(KC)], [(norm, i) for i in range(w // P)]
 
         def mask(b, a):
             blk = st[b]["kc"][:, a, P * a : P * a + P]
@@ -196,18 +220,27 @@ def tile_k_attention_ex_t_kernel(tc, x, r_sigma, margin, out):
                 grp_of[b, a] = eight.tile([P, NG, P, PACK], BF16, name="grp", tag="grp", align_bytes=64)
             return grp_of[b, a]
 
-        def mirror(b, a):
+        def mirror_ops(b, a):
             kc, lo = st[b]["kc"], P * a
             if a == NT - 1:
-                return
-            kt = psum_w.tile([P, NT, P], BF16, name="kt", tag="w")
-            for s in range(a + 1, NT):
-                nc.tensor.transpose(kt[:, s, :], kc[:, a, P * s : P * s + P], ident[:])
+                return []
             end = PACK * (a // PACK) + PACK
-            if a + 1 < end:
-                nc.scalar.copy(out=kc[:, a + 1 : end, lo : lo + P], in_=kt[:, a + 1 : end, :])
-            if end < NT:
-                nc.scalar.copy(out=group(b, a)[:, 1], in_=kt[:, end:NT, :].rearrange("p j t -> p t j"))
+            box = []
+
+            def one(s):
+                if s == a + 1:
+                    kt = psum_w.tile([P, NT, P], BF16, name="kt", tag="w")
+                    box.append(kt)
+                kt = box[0]
+                nc.tensor.transpose(kt[:, s, :], kc[:, a, P * s : P * s + P], ident[:])
+                if s == end - 1 and a + 1 < end and end == NT:
+                    nc.scalar.copy(out=kc[:, a + 1 : end, lo : lo + P], in_=kt[:, a + 1 : end, :])
+                if s == NT - 1 and end < NT:
+                    if a + 1 < end:
+                        nc.scalar.copy(out=kc[:, a + 1 : end, lo : lo + P], in_=kt[:, a + 1 : end, :])
+                    nc.scalar.copy(out=group(b, a)[:, 1], in_=kt[:, end:NT, :].rearrange("p j t -> p t j"))
+
+            return [(one, s) for s in range(a + 1, NT)]
 
         def regroup(b, a, g, copy):
             copy(
@@ -256,30 +289,37 @@ def tile_k_attention_ex_t_kernel(tc, x, r_sigma, margin, out):
                 wp = psum_w.tile([P, BANK], F32, name="wp", tag="w")
                 nc.tensor.matmul(wp[:], lhsT=zeros[:, 0:P], rhs=zeros[:], start=True, stop=True)
             for a in range(NT):
-                x_transpose(0, a, nc.scalar.copy if a % 2 else nc.vector.tensor_copy)
+                run(x_ops(0, a, nc.scalar.copy if a % 2 else nc.vector.tensor_copy))
             for a in range(NT):
                 if a % 2:
                     square_s(0, a)
                 else:
                     square_v(0, a)
-            for bank in banks[:HEAD]:
-                gram_open(*bank)
+            first = [gram_ops(*bank) for bank in banks[:HEAD]]
+            for chunks, folds in first:
+                run(chunks)
             for i in range(6):
                 norm_step(0, i)
-            norm_rows(0)
-            for bank in banks[:HEAD]:
-                gram_close(*bank)
+            run(norm_ops(0))
+            for chunks, folds in first:
+                run(folds)
             for g in range(NG):
                 x_regroup(0, g)
                 x_quantize(0, g)
             mask(0, 0)
             done = [HEAD]
 
-            def next_bank(row):
-                if done[0] < min(len(banks), last_bank[row] + LEAD):
-                    gram_open(*banks[done[0]])
-                    gram_close(*banks[done[0]])
-                    done[0] += 1
+            def weave(products, turns):
+                k = 0
+                for q, op in enumerate(products):
+                    run([op])
+                    left = len(products) - 1 - q
+                    while k < len(turns) and left > 0:
+                        run([turns[k]])
+                        k += 1
+                        if len(turns) - k <= left - 1:
+                            break
+                run(turns[k:])
 
             n = len(rows)
             for i in range(-1, n + 1):
@@ -290,17 +330,24 @@ def tile_k_attention_ex_t_kernel(tc, x, r_sigma, margin, out):
                 if prep and cur[1] == 0:
                     alloc(prep)
                 spread = prep and cur[1] in (1, 2)
-                next_bank(tgt)
-                if nxt and nxt < (B - 1, NT - 2):
-                    mirror(*nxt)
-                if nxt == (B - 1, NT - 3):
-                    mirror(B - 1, NT - 2)
-                if prep and cur[1] < 4:
-                    x_transpose(prep, 2 * cur[1], nc.scalar.copy)
-                    x_transpose(prep, 2 * cur[1] + 1, nc.scalar.copy)
+                sp = 3 * cur[1] - 3 if spread else 0
+                turns = []
                 if prep and cur[1] == 3:
-                    norm_rows(prep)
-                next_bank(tgt)
+                    turns += norm_ops(prep)
+                if nxt and nxt < (B - 1, NT - 2):
+                    turns += mirror_ops(*nxt)
+                if nxt == (B - 1, NT - 3):
+                    turns += mirror_ops(B - 1, NT - 2)
+                if prep and cur[1] < 4:
+                    turns += x_ops(prep, 2 * cur[1], nc.scalar.copy)
+                    turns += x_ops(prep, 2 * cur[1] + 1, nc.scalar.copy)
+                goal = min(len(banks), last_bank[tgt] + LEAD)
+                products = []
+                while done[0] < goal:
+                    chunks, folds = gram_ops(*banks[done[0]])
+                    products += chunks + folds
+                    done[0] += 1
+                weave(products, turns)
                 if nxt:
                     b, a = nxt
                     if b < B - 1:
@@ -312,17 +359,17 @@ def tile_k_attention_ex_t_kernel(tc, x, r_sigma, margin, out):
                             regroup(b, 2 * a - 4, 0, nc.scalar.copy)
                             regroup(b, 2 * a - 3, 0, nc.scalar.copy)
                 if spread:
-                    norm_step(prep, 3 * cur[1] - 3)
+                    norm_step(prep, sp)
                 if i + 2 < n:
                     mask(*rows[i + 2])
                 if i >= 1:
                     finish(*rows[i - 1])
                 if spread:
-                    norm_step(prep, 3 * cur[1] - 2)
+                    norm_step(prep, sp + 1)
                 if nxt:
                     k_quantize(*nxt)
                 if spread:
-                    norm_step(prep, 3 * cur[1] - 1)
+                    norm_step(prep, sp + 2)
                 if cur:
                     multiply(*cur)
                 if prep and cur[1] == 0:
@@ -335,4 +382,3 @@ def tile_k_attention_ex_t_kernel(tc, x, r_sigma, margin, out):
                     x_regroup(prep, cur[1] - 1)
                 if prep and cur[1] in (6, 7):
                     x_quantize(prep, cur[1] - 6)
-                next_bank(tgt)

@@ -59,8 +59,6 @@ def tile_k_attention_ex_t_kernel(tc, x, r_sigma, margin, out):
         nc.vector.memset(zeros[:], 0.0)
         ident = const.tile([P, P], BF16, name="ident")
         make_identity(nc, ident[:])
-        ident_f = const.tile([P, P], F32, name="ident_f")
-        make_identity(nc, ident_f[:])
         offdiag = const.tile([P, P], BF16, name="offdiag")
         nc.vector.tensor_scalar(out=offdiag[:], in0=ident[:], scalar1=-1.0, scalar2=1.0, op0=ALU.mult, op1=ALU.add)
         ones = const.tile([P, P], BF16, name="ones")
@@ -116,22 +114,18 @@ def tile_k_attention_ex_t_kernel(tc, x, r_sigma, margin, out):
             )
 
         def x_ops(b, a, copy):
-            words = x_sb[b][:, a, :].bitcast(F32)
             box = []
 
-            def one(h):
-                if h == 0:
-                    tp = psum_w.tile([P, KC // 2, P], F32, name="tp", tag="w")
+            def one(k):
+                if k == 0:
+                    tp = psum_w.tile([P, KC, P], BF16, name="tp", tag="w")
                     box.append(tp)
                 tp = box[0]
-                nc.tensor.transpose(tp[:, h, :], words[:, P * h : P * h + P], ident_f[:])
-                if h == KC // 2 - 1:
-                    copy(
-                        out=st[b]["xT"][:].rearrange("p (h e) t -> p h e t", e=2)[:, :, :, P * a : P * a + P],
-                        in_=tp[:].bitcast(BF16).rearrange("p h (t e) -> p h e t", e=2),
-                    )
+                nc.tensor.transpose(tp[:, k, :], x_sb[b][:, a, P * k : P * k + P], ident[:])
+                if k == KC - 1:
+                    copy(out=st[b]["xT"][:, :, P * a : P * a + P], in_=tp[:])
 
-            return [(one, h) for h in range(KC // 2)]
+            return [(one, k) for k in range(KC)]
 
         def run(ops):
             for f, q in ops:
@@ -372,7 +366,10 @@ def tile_k_attention_ex_t_kernel(tc, x, r_sigma, margin, out):
                     norm_step(prep, sp + 2)
                 if cur:
                     multiply(*cur)
-                if prep and cur[1] == 0:
+                if cur and cur[1] >= PACK and cur[0] + 2 < B:
+                    square_s(cur[0] + 2, 2 * cur[1] - NT)
+                    square_s(cur[0] + 2, 2 * cur[1] - NT + 1)
+                if prep == 1 and cur[1] == 0:
                     for a in range(NT):
                         if a < V_SQUARES:
                             square_v(prep, a)

@@ -22,7 +22,7 @@ BANK = 512
 LEAD = 3
 HEAD = 4
 
-WARM = 6
+WARM = 16
 V_SQUARES = 5
 
 FLOPS = 2 * (2 * B * T * T * C)
@@ -39,34 +39,30 @@ def tile_k_attention_ex_t_kernel(tc, x, r_sigma, margin, out):
         psum_w = ctx.enter_context(tc.psum_pool(name="psum_w", bufs=6))
         psum_o = ctx.enter_context(tc.psum_pool(name="psum_o", bufs=2))
 
+        zeros = const.tile([P, P], BF16, name="zeros")
+        nc.vector.memset(zeros[:], 0.0)
         r_bf = const.tile([P, 1], BF16, name="r_bf")
         m_bf = const.tile([P, 1], BF16, name="m_bf")
-        nc.scalar.dma_start(out=r_bf[:], in_=r_sigma.partition_broadcast(P))
-        nc.scalar.dma_start(out=m_bf[:], in_=margin.partition_broadcast(P))
 
         x_tok = x.rearrange("b (g p j) c -> b g p j c", p=P, j=PACK)
         out_tok = out.rearrange("b (g p j) c -> b g p j c", p=P, j=PACK)
         x_sb = []
         for b in range(B):
             xb = xin.tile([P, NT, C], BF16, name="xb", tag="xb")
-            n = PACK // 2 if b == 0 else PACK
-            for lo in range(0, NT, n):
+            for lo, n in ((0, 1), (1, 1), (2, 2), (4, 2), (6, 2)) if b == 0 else ((0, PACK), (PACK, PACK)):
                 g, j = divmod(lo, PACK)
                 nc.sync.dma_start(out=xb[:, lo : lo + n, :], in_=x_tok[b, g, :, j : j + n, :])
             x_sb.append(xb)
+            if b == 0:
+                nc.sync.dma_start(out=r_bf[:], in_=r_sigma.partition_broadcast(P))
+                nc.sync.dma_start(out=m_bf[:], in_=margin.partition_broadcast(P))
 
-        zeros = const.tile([P, BANK], BF16, name="zeros")
-        nc.vector.memset(zeros[:], 0.0)
         ident = const.tile([P, P], BF16, name="ident")
         make_identity(nc, ident[:])
         offdiag = const.tile([P, P], BF16, name="offdiag")
         nc.vector.tensor_scalar(out=offdiag[:], in0=ident[:], scalar1=-1.0, scalar2=1.0, op0=ALU.mult, op1=ALU.add)
         ones = const.tile([P, P], BF16, name="ones")
         nc.vector.memset(ones[:], 1.0)
-        two_r = const.tile([P, 1], F32, name="two_r")
-        nc.vector.tensor_scalar(out=two_r[:], in0=r_bf[:], scalar1=2.0, scalar2=None, op0=ALU.mult)
-        m_f = const.tile([P, 1], F32, name="m_f")
-        nc.vector.tensor_copy(out=m_f[:], in_=m_bf[:])
         warm = const.tile([P, 1], F32, name="warm")
         nc.scalar.activation(out=warm[:], in_=ones[:, 0:1], func=ACT.Exp)
         pieces = []
@@ -79,8 +75,13 @@ def tile_k_attention_ex_t_kernel(tc, x, r_sigma, margin, out):
             out=rowsum[:], in_=ident[:, 0 : 3 * NT].rearrange("p (a i) -> p a i", i=3), axis=AX.X, op=ALU.add
         )
         pick = const.tile([P, NT, P], BF16, name="pick")
-        nc.vector.tensor_copy(out=pick[:], in_=rowsum[:].unsqueeze(2).to_broadcast([P, NT, P]))
+        nc.vector.tensor_scalar(
+            out=pick[:], in0=rowsum[:].unsqueeze(2).to_broadcast([P, NT, P]), scalar1=-0.5, scalar2=None, op0=ALU.mult
+        )
 
+        two_r = const.tile([P, 1], F32, name="two_r")
+        minus_r = const.tile([P, 1], F32, name="minus_r")
+        m_f = const.tile([P, 1], F32, name="m_f")
         sq_of = []
         for b in range(B):
             sq = const.tile([P, NT], F32, name="sq%d" % b)
@@ -89,7 +90,6 @@ def tile_k_attention_ex_t_kernel(tc, x, r_sigma, margin, out):
 
         def alloc(b):
             st[b] = {
-                "half": two.tile([P, NT], F32, name="half", tag="half"),
                 "rest": two.tile([P, NT], F32, name="rest", tag="rest"),
                 "bias": two.tile([P, NT], F32, name="bias", tag="bias"),
                 "xT": two.tile([P, KC, T], BF16, name="xT", tag="xT"),
@@ -132,22 +132,20 @@ def tile_k_attention_ex_t_kernel(tc, x, r_sigma, margin, out):
                 f(q)
 
         def norm_step(b, i):
-            d = st[b]
+            d, sq = st[b], sq_of[b][:]
             u = pieces[b % 2][:, 0 : 3 * NT].rearrange("p (a i) -> p a i", i=3)
-            half, rest = d["half"][:], d["rest"][:]
+            rest = d["rest"][:]
             if i == 0:
-                nc.vector.tensor_scalar(out=half, in0=sq_of[b][:], scalar1=-0.5, scalar2=None, op0=ALU.mult)
+                nc.vector.tensor_copy(out=u[:, :, 0], in_=sq)
             elif i == 1:
-                nc.vector.tensor_copy(out=u[:, :, 0], in_=half)
+                nc.vector.tensor_tensor(out=rest, in0=sq, in1=u[:, :, 0], op=ALU.subtract)
             elif i == 2:
-                nc.vector.tensor_tensor(out=rest, in0=half, in1=u[:, :, 0], op=ALU.subtract)
-            elif i == 3:
                 nc.vector.tensor_copy(out=u[:, :, 1], in_=rest)
-            elif i == 4:
+            elif i == 3:
                 nc.vector.tensor_tensor(out=u[:, :, 2], in0=rest, in1=u[:, :, 1], op=ALU.subtract)
-            else:
+            elif i == 4:
                 nc.vector.tensor_scalar(
-                    out=d["bias"][:], in0=half, scalar1=two_r[:], scalar2=m_f[:], op0=ALU.mult, op1=ALU.add
+                    out=d["bias"][:], in0=sq, scalar1=minus_r[:], scalar2=m_f[:], op0=ALU.mult, op1=ALU.add
                 )
 
         def norm_ops(b):
@@ -279,20 +277,29 @@ def tile_k_attention_ex_t_kernel(tc, x, r_sigma, margin, out):
         with ExitStack() as pinned:
             pinned.enter_context(tc.manual_schedule())
             alloc(0)
+            wp = psum_o.tile([P, BANK], F32, name="wp", tag="o")
+
+            def warm_up():
+                nc.tensor.matmul(wp[:, 0:P], lhsT=zeros[:], rhs=zeros[:], start=True, stop=True)
+
             for i in range(WARM):
-                wp = psum_w.tile([P, BANK], F32, name="wp", tag="w")
-                nc.tensor.matmul(wp[:], lhsT=zeros[:, 0:P], rhs=zeros[:], start=True, stop=True)
+                warm_up()
             for a in range(NT):
-                run(x_ops(0, a, nc.scalar.copy if a % 2 else nc.vector.tensor_copy))
+                for op in x_ops(0, a, nc.scalar.copy if a % 2 else nc.vector.tensor_copy):
+                    run([op])
+                    warm_up()
             for a in range(NT):
                 if a % 2:
                     square_s(0, a)
                 else:
                     square_v(0, a)
+            nc.vector.tensor_scalar(out=two_r[:], in0=r_bf[:], scalar1=2.0, scalar2=None, op0=ALU.mult)
+            nc.vector.tensor_scalar(out=minus_r[:], in0=r_bf[:], scalar1=-1.0, scalar2=None, op0=ALU.mult)
+            nc.vector.tensor_copy(out=m_f[:], in_=m_bf[:])
             first = [gram_ops(*bank) for bank in banks[:HEAD]]
             for chunks, folds in first:
                 run(chunks)
-            for i in range(6):
+            for i in range(5):
                 norm_step(0, i)
             run(norm_ops(0))
             for chunks, folds in first:

@@ -23,7 +23,10 @@ LEAD = 3
 HEAD = 4
 
 WARM = 16
-V_SQUARES = 5
+V_SQUARES = 4
+HEAD_SQUARES = (5, 6, 7)
+AHEAD_2 = {5: (0,), 6: (1,), 7: (2, 3)}
+AHEAD_1 = {0: (4,), 1: (5,), 2: (6,), 3: (7,)}
 
 FLOPS = 2 * (2 * B * T * T * C)
 
@@ -92,13 +95,17 @@ def tile_k_attention_ex_t_kernel(tc, x, r_sigma, margin, out):
             st[b] = {
                 "rest": two.tile([P, NT], F32, name="rest", tag="rest"),
                 "bias": two.tile([P, NT], F32, name="bias", tag="bias"),
-                "xT": two.tile([P, KC, T], BF16, name="xT", tag="xT"),
                 "rows": two.tile([P, P], BF16, name="rows", tag="rows"),
                 "xg": two.tile([P, NG, C, PACK], BF16, name="xg", tag="xg", align_bytes=64),
                 "xq": two.tile([P, NG, C], U32, name="xq", tag="xq", align_bytes=64),
                 "xs": two.tile([P, NG, C], U8, name="xs", tag="xs", align_bytes=64),
                 "kc": two.tile([P, NT, T], BF16, name="kc", tag="kc"),
             }
+
+        xT_of = {}
+
+        def alloc_xT(b):
+            xT_of[b] = two.tile([P, KC, T], BF16, name="xT", tag="xT")
 
         def square_s(b, a):
             junk = two.tile([P, C], BF16, name="junk", tag="junk")
@@ -123,7 +130,7 @@ def tile_k_attention_ex_t_kernel(tc, x, r_sigma, margin, out):
                 tp = box[0]
                 nc.tensor.transpose(tp[:, k, :], x_sb[b][:, a, P * k : P * k + P], ident[:])
                 if k == KC - 1:
-                    copy(out=st[b]["xT"][:, :, P * a : P * a + P], in_=tp[:])
+                    copy(out=xT_of[b][:, :, P * a : P * a + P], in_=tp[:])
 
             return [(one, k) for k in range(KC)]
 
@@ -174,7 +181,7 @@ def tile_k_attention_ex_t_kernel(tc, x, r_sigma, margin, out):
 
         def gram_ops(b, a, c0):
             w = min(BANK, T - c0)
-            xT = st[b]["xT"]
+            xT = xT_of[b]
             box = []
 
             def chunk(k):
@@ -277,6 +284,8 @@ def tile_k_attention_ex_t_kernel(tc, x, r_sigma, margin, out):
         with ExitStack() as pinned:
             pinned.enter_context(tc.manual_schedule())
             alloc(0)
+            alloc_xT(0)
+            alloc_xT(1)
             wp = psum_o.tile([P, BANK], F32, name="wp", tag="o")
 
             def warm_up():
@@ -299,6 +308,8 @@ def tile_k_attention_ex_t_kernel(tc, x, r_sigma, margin, out):
             first = [gram_ops(*bank) for bank in banks[:HEAD]]
             for chunks, folds in first:
                 run(chunks)
+            for a in HEAD_SQUARES:
+                square_s(1, a)
             for i in range(5):
                 norm_step(0, i)
             run(norm_ops(0))
@@ -333,15 +344,24 @@ def tile_k_attention_ex_t_kernel(tc, x, r_sigma, margin, out):
                 spread = prep and cur[1] in (1, 2)
                 sp = 3 * cur[1] - 3 if spread else 0
                 turns = []
-                if prep and cur[1] == 3:
+                if prep and cur[1] == 4:
                     turns += norm_ops(prep)
                 if nxt and nxt < (B - 1, NT - 2):
                     turns += mirror_ops(*nxt)
                 if nxt == (B - 1, NT - 3):
                     turns += mirror_ops(B - 1, NT - 2)
-                if prep and cur[1] < 4:
-                    turns += x_ops(prep, 2 * cur[1], nc.scalar.copy)
-                    turns += x_ops(prep, 2 * cur[1] + 1, nc.scalar.copy)
+                if prep == 1:
+                    ahead = [(1, q) for q in (2 * cur[1], 2 * cur[1] + 1) if q < NT]
+                elif prep:
+                    ahead = [(prep, q) for q in AHEAD_1.get(cur[1], ())]
+                else:
+                    ahead = []
+                if cur and cur[0] + 2 < B:
+                    if cur[1] == 5:
+                        alloc_xT(cur[0] + 2)
+                    ahead += [(cur[0] + 2, q) for q in AHEAD_2.get(cur[1], ())]
+                for b, a in ahead:
+                    turns += x_ops(b, a, nc.scalar.copy)
                 goal = min(len(banks), last_bank[tgt] + LEAD)
                 products = []
                 while done[0] < goal:
@@ -380,9 +400,9 @@ def tile_k_attention_ex_t_kernel(tc, x, r_sigma, margin, out):
                     for a in range(NT):
                         if a < V_SQUARES:
                             square_v(prep, a)
-                        else:
+                        elif a not in HEAD_SQUARES:
                             square_s(prep, a)
-                if prep and cur[1] in (1, 2):
-                    x_regroup(prep, cur[1] - 1)
+                if prep and cur[1] in (5, 6):
+                    x_regroup(prep, cur[1] - 5)
                 if prep and cur[1] in (6, 7):
                     x_quantize(prep, cur[1] - 6)

@@ -97,8 +97,8 @@ def tile_k_attention_ex_t_kernel(tc, x, r_sigma, margin, out):
                 "bias": two.tile([P, NT], F32, name="bias", tag="bias"),
                 "rows": two.tile([P, P], BF16, name="rows", tag="rows"),
                 "xg": two.tile([P, NG, C, PACK], BF16, name="xg", tag="xg", align_bytes=64),
-                "xq": two.tile([P, NG, C], U32, name="xq", tag="xq", align_bytes=64),
-                "xs": two.tile([P, NG, C], U8, name="xs", tag="xs", align_bytes=64),
+                "xq": two.tile([P, NG, C], U32, name="xq", tag="xq", align_bytes=256),
+                "xs": two.tile([P, NG, C], U8, name="xs", tag="xs", align_bytes=256),
                 "kc": two.tile([P, NT, T], BF16, name="kc", tag="kc"),
             }
 
@@ -248,8 +248,8 @@ def tile_k_attention_ex_t_kernel(tc, x, r_sigma, margin, out):
             )
 
         def k_quantize(b, a):
-            kq = four.tile([P, NG, P], U32, name="kq", tag="kq", align_bytes=64)
-            ks = four.tile([P, NG, P], U8, name="ks", tag="ks", align_bytes=64)
+            kq = four.tile([P, NG, P], U32, name="kq", tag="kq", align_bytes=256)
+            ks = four.tile([P, NG, P], U8, name="ks", tag="ks", align_bytes=256)
             codes_of[b, a] = (kq, ks)
             nc.vector.quantize_mx(
                 out=kq[:].rearrange("p g t -> p (g t)").bitcast(FP8X4),

@@ -19,12 +19,12 @@ KC = C // P
 PACK = 4
 NG = T // (P * PACK)
 BANK = 512
+HALVES = (2, 1, 1, 1)
 LEAD = 3
-HEAD = 4
+LEAD_FIRST = 4
 
 WARM = 16
-V_SQUARES = 4
-HEAD_SQUARES = (5, 6, 7)
+X_SECOND = {-1: (1,), 0: (2,), 1: (3, 4), 2: (5, 6), 3: (7,)}
 AHEAD_2 = {5: (0,), 6: (1,), 7: (2, 3)}
 AHEAD_1 = {0: (4,), 1: (5,), 2: (6,), 3: (7,)}
 
@@ -50,15 +50,14 @@ def tile_k_attention_ex_t_kernel(tc, x, r_sigma, margin, out):
         x_tok = x.rearrange("b (g p j) c -> b g p j c", p=P, j=PACK)
         out_tok = out.rearrange("b (g p j) c -> b g p j c", p=P, j=PACK)
         x_sb = []
+        nc.scalar.dma_start(out=r_bf[:], in_=r_sigma.partition_broadcast(P))
+        nc.scalar.dma_start(out=m_bf[:], in_=margin.partition_broadcast(P))
         for b in range(B):
             xb = xin.tile([P, NT, C], BF16, name="xb", tag="xb")
             for lo, n in ((0, 1), (1, 1), (2, 2), (4, 2), (6, 2)) if b == 0 else ((0, PACK), (PACK, PACK)):
                 g, j = divmod(lo, PACK)
                 nc.sync.dma_start(out=xb[:, lo : lo + n, :], in_=x_tok[b, g, :, j : j + n, :])
             x_sb.append(xb)
-            if b == 0:
-                nc.sync.dma_start(out=r_bf[:], in_=r_sigma.partition_broadcast(P))
-                nc.sync.dma_start(out=m_bf[:], in_=margin.partition_broadcast(P))
 
         ident = const.tile([P, P], BF16, name="ident")
         make_identity(nc, ident[:])
@@ -95,7 +94,6 @@ def tile_k_attention_ex_t_kernel(tc, x, r_sigma, margin, out):
             st[b] = {
                 "rest": two.tile([P, NT], F32, name="rest", tag="rest"),
                 "bias": two.tile([P, NT], F32, name="bias", tag="bias"),
-                "rows": two.tile([P, P], BF16, name="rows", tag="rows"),
                 "xg": two.tile([P, NG, C, PACK], BF16, name="xg", tag="xg", align_bytes=64),
                 "xq": two.tile([P, NG, C], U32, name="xq", tag="xq", align_bytes=256),
                 "xs": two.tile([P, NG, C], U8, name="xs", tag="xs", align_bytes=256),
@@ -138,30 +136,33 @@ def tile_k_attention_ex_t_kernel(tc, x, r_sigma, margin, out):
             for f, q in ops:
                 f(q)
 
-        def norm_step(b, i):
-            d, sq = st[b], sq_of[b][:]
-            u = pieces[b % 2][:, 0 : 3 * NT].rearrange("p (a i) -> p a i", i=3)
-            rest = d["rest"][:]
+        rows_of = {}
+
+        def norm_step(b, half, i):
+            n = NT // HALVES[b]
+            cols = slice(n * half, n * half + n)
+            sq = sq_of[b][:, cols]
+            u = pieces[b % 2][:, 0 : 3 * NT].rearrange("p (a i) -> p a i", i=3)[:, cols]
+            rest = st[b]["rest"][:, cols]
             if i == 0:
                 nc.vector.tensor_copy(out=u[:, :, 0], in_=sq)
             elif i == 1:
-                nc.vector.tensor_tensor(out=rest, in0=sq, in1=u[:, :, 0], op=ALU.subtract)
+                nc.vector.tensor_tensor(out=u[:, :, 1], in0=sq, in1=u[:, :, 0], op=ALU.subtract)
             elif i == 2:
-                nc.vector.tensor_copy(out=u[:, :, 1], in_=rest)
+                nc.vector.tensor_tensor(out=rest, in0=sq, in1=u[:, :, 0], op=ALU.subtract)
             elif i == 3:
                 nc.vector.tensor_tensor(out=u[:, :, 2], in0=rest, in1=u[:, :, 1], op=ALU.subtract)
             elif i == 4:
                 nc.vector.tensor_scalar(
-                    out=d["bias"][:], in0=sq, scalar1=minus_r[:], scalar2=m_f[:], op0=ALU.mult, op1=ALU.add
+                    out=st[b]["bias"][:, cols], in0=sq, scalar1=minus_r[:], scalar2=m_f[:], op0=ALU.mult, op1=ALU.add
                 )
 
-        def norm_ops(b):
-            def one(q):
-                tp = psum_w.tile([P, P], BF16, name="tpr", tag="w")
-                nc.tensor.transpose(tp[:], pieces[b % 2][:], ident[:])
-                nc.scalar.copy(out=st[b]["rows"][:], in_=tp[:])
-
-            return [(one, 0)]
+        def norm_rows(b, half):
+            rt = two.tile([P, P], BF16, name="rows%d" % half, tag="rows%d" % half)
+            rows_of[b, half] = rt
+            tp = psum_w.tile([P, P], BF16, name="tpr", tag="w")
+            nc.tensor.transpose(tp[:], pieces[b % 2][:], ident[:])
+            nc.scalar.copy(out=rt[:], in_=tp[:])
 
         def x_regroup(b, g):
             nc.vector.tensor_copy(
@@ -177,14 +178,11 @@ def tile_k_attention_ex_t_kernel(tc, x, r_sigma, margin, out):
                 in_=d["xg"][:, g].rearrange("p c j -> p (c j)"),
             )
 
-        gp_of = {}
-
-        def gram_ops(b, a, c0):
-            w = min(BANK, T - c0)
-            xT = xT_of[b]
+        def gram_ops(b, a, c0, w):
             box = []
 
             def chunk(k):
+                xT = xT_of[b]
                 if k == 0:
                     gp = psum_w.tile([P, BANK], F32, name="gp", tag="w")
                     box.append(gp)
@@ -198,7 +196,8 @@ def tile_k_attention_ex_t_kernel(tc, x, r_sigma, margin, out):
                 gp = box[0]
                 last = i == w // P - 1
                 nc.tensor.matmul(
-                    gp[:, P * i : P * i + P], lhsT=pick[:, c0 // P + i, :], rhs=d["rows"][:], start=False, stop=last
+                    gp[:, P * i : P * i + P], lhsT=pick[:, c0 // P + i, :],
+                    rhs=rows_of[b, min(c0 // BANK, HALVES[b] - 1)][:], start=False, stop=last,
                 )
                 if last:
                     nc.scalar.activation(
@@ -276,9 +275,13 @@ def tile_k_attention_ex_t_kernel(tc, x, r_sigma, margin, out):
             nc.sync.dma_start(out=out_tok[b, a // PACK, :, a % PACK, :], in_=res[:])
 
         rows = [(b, a) for b in range(B) for a in range(NT)]
-        banks = [(b, a, c0) for b, a in rows for c0 in range(P * a, T, BANK)]
+        banks = []
+        for a in (0, 2):
+            banks += [(0, q, P * q, BANK - P * q) for q in (a, a + 1)] + [(0, q, BANK, BANK) for q in (a, a + 1)]
+        banks += [(0, a, P * a, T - P * a) for a in range(PACK, NT)]
+        banks += [(b, a, c0, min(BANK, T - c0)) for b, a in rows if b for c0 in range(P * a, T, BANK)]
         last_bank = {}
-        for i, (b, a, c0) in enumerate(banks):
+        for i, (b, a, c0, w) in enumerate(banks):
             last_bank[b, a] = i + 1
 
         with ExitStack() as pinned:
@@ -294,32 +297,42 @@ def tile_k_attention_ex_t_kernel(tc, x, r_sigma, margin, out):
             for i in range(WARM):
                 warm_up()
             for a in range(NT):
-                for op in x_ops(0, a, nc.scalar.copy if a % 2 else nc.vector.tensor_copy):
+                for op in x_ops(0, a, nc.scalar.copy):
                     run([op])
                     warm_up()
-            for a in range(NT):
-                if a % 2:
-                    square_s(0, a)
-                else:
-                    square_v(0, a)
+            for a in range(PACK):
+                square_v(0, a)
             nc.vector.tensor_scalar(out=two_r[:], in0=r_bf[:], scalar1=2.0, scalar2=None, op0=ALU.mult)
             nc.vector.tensor_scalar(out=minus_r[:], in0=r_bf[:], scalar1=-1.0, scalar2=None, op0=ALU.mult)
             nc.vector.tensor_copy(out=m_f[:], in_=m_bf[:])
-            first = [gram_ops(*bank) for bank in banks[:HEAD]]
-            for chunks, folds in first:
-                run(chunks)
-            for a in HEAD_SQUARES:
-                square_s(1, a)
+            first = [gram_ops(*bank) for bank in banks[:PACK]]
+            run(first[0][0])
             for i in range(5):
-                norm_step(0, i)
-            run(norm_ops(0))
-            for chunks, folds in first:
-                run(folds)
+                norm_step(0, 0, i)
+            square_s(0, 4)
+            for a in (5, 6, 7):
+                square_v(0, a)
+            norm_rows(0, 0)
+            square_s(1, 0)
+            run(first[1][0])
+            for i in range(5):
+                norm_step(0, 1, i)
+            run(first[0][1])
+            run(first[1][1])
+            run(first[2][0])
+            norm_rows(0, 1)
+            square_s(1, 1)
+            square_s(1, 2)
+            run(first[3][0])
+            run(first[2][1])
+            run(first[3][1])
             for g in range(NG):
                 x_regroup(0, g)
                 x_quantize(0, g)
+            square_v(1, 3)
+            square_v(1, 4)
             mask(0, 0)
-            done = [HEAD]
+            done = [PACK]
 
             def weave(products, turns):
                 k = 0
@@ -333,6 +346,9 @@ def tile_k_attention_ex_t_kernel(tc, x, r_sigma, margin, out):
                             break
                 run(turns[k:])
 
+            chunks, folds = gram_ops(*banks[PACK])
+            weave(chunks + folds, x_ops(1, 0, nc.scalar.copy))
+            done[0] += 1
             n = len(rows)
             for i in range(-1, n + 1):
                 cur = rows[i] if 0 <= i < n else None
@@ -345,14 +361,14 @@ def tile_k_attention_ex_t_kernel(tc, x, r_sigma, margin, out):
                 sp = 3 * cur[1] - 3 if spread else 0
                 turns = []
                 if prep and cur[1] == 4:
-                    turns += norm_ops(prep)
+                    turns += [(lambda q: norm_rows(q, 0), prep)]
                 if nxt and nxt < (B - 1, NT - 2):
                     turns += mirror_ops(*nxt)
                 if nxt == (B - 1, NT - 3):
                     turns += mirror_ops(B - 1, NT - 2)
-                if prep == 1:
-                    ahead = [(1, q) for q in (2 * cur[1], 2 * cur[1] + 1) if q < NT]
-                elif prep:
+                if i in X_SECOND:
+                    ahead = [(1, q) for q in X_SECOND[i]]
+                elif prep and prep > 1:
                     ahead = [(prep, q) for q in AHEAD_1.get(cur[1], ())]
                 else:
                     ahead = []
@@ -362,7 +378,7 @@ def tile_k_attention_ex_t_kernel(tc, x, r_sigma, margin, out):
                     ahead += [(cur[0] + 2, q) for q in AHEAD_2.get(cur[1], ())]
                 for b, a in ahead:
                     turns += x_ops(b, a, nc.scalar.copy)
-                goal = min(len(banks), last_bank[tgt] + LEAD)
+                goal = min(len(banks), last_bank[tgt] + (LEAD_FIRST if i < 2 else LEAD))
                 products = []
                 while done[0] < goal:
                     chunks, folds = gram_ops(*banks[done[0]])
@@ -376,32 +392,28 @@ def tile_k_attention_ex_t_kernel(tc, x, r_sigma, margin, out):
                             regroup(b, a, g, nc.vector.tensor_copy)
                     else:
                         regroup(b, a, a // PACK, nc.scalar.copy if a > 5 else nc.vector.tensor_copy)
-                        if a in (4, 5):
-                            regroup(b, 2 * a - 4, 0, nc.scalar.copy)
-                            regroup(b, 2 * a - 3, 0, nc.scalar.copy)
+                        for q in {4: (4, 5), 5: (6, 7)}.get(a, ()):
+                            regroup(b, q, 0, nc.scalar.copy)
                 if spread:
-                    norm_step(prep, sp)
+                    norm_step(prep, 0, sp)
                 if i + 2 < n:
                     mask(*rows[i + 2])
                 if i >= 1:
                     finish(*rows[i - 1])
                 if spread:
-                    norm_step(prep, sp + 1)
+                    norm_step(prep, 0, sp + 1)
                 if nxt:
                     k_quantize(*nxt)
                 if spread:
-                    norm_step(prep, sp + 2)
+                    norm_step(prep, 0, sp + 2)
                 if cur:
                     multiply(*cur)
                 if cur and cur[1] >= PACK and cur[0] + 2 < B:
                     square_s(cur[0] + 2, 2 * cur[1] - NT)
                     square_s(cur[0] + 2, 2 * cur[1] - NT + 1)
-                if prep == 1 and cur[1] == 0:
-                    for a in range(NT):
-                        if a < V_SQUARES:
-                            square_v(prep, a)
-                        elif a not in HEAD_SQUARES:
-                            square_s(prep, a)
+                if i in (-1, 0):
+                    for a in ((5, 6), (7,))[i + 1]:
+                        square_v(1, a)
                 if prep and cur[1] in (5, 6):
                     x_regroup(prep, cur[1] - 5)
                 if prep and cur[1] in (6, 7):

@@ -44,14 +44,14 @@ def tile_k_attention_ex_t_kernel(tc, x, r_sigma, margin, out):
 
         zeros = const.tile([P, P], BF16, name="zeros")
         nc.vector.memset(zeros[:], 0.0)
-        r_bf = const.tile([P, 1], BF16, name="r_bf")
-        m_bf = const.tile([P, 1], BF16, name="m_bf")
+        rm = const.tile([P, 32], BF16, name="rm")
+        nc.vector.memset(rm[:], 0.0)
 
         x_tok = x.rearrange("b (g p j) c -> b g p j c", p=P, j=PACK)
         out_tok = out.rearrange("b (g p j) c -> b g p j c", p=P, j=PACK)
         x_sb = []
-        nc.scalar.dma_start(out=r_bf[:], in_=r_sigma.partition_broadcast(P))
-        nc.scalar.dma_start(out=m_bf[:], in_=margin.partition_broadcast(P))
+        nc.scalar.dma_start(out=rm[0:1, 0:1], in_=r_sigma.rearrange("(a b) -> a b", a=1))
+        nc.scalar.dma_start(out=rm[0:1, 16:17], in_=margin.rearrange("(a b) -> a b", a=1))
         for b in range(B):
             xb = xin.tile([P, NT, C], BF16, name="xb", tag="xb")
             for lo, n in ((0, 1), (1, 1), (2, 2), (4, 2), (6, 2)) if b == 0 else ((0, PACK), (PACK, PACK)):
@@ -302,16 +302,19 @@ def tile_k_attention_ex_t_kernel(tc, x, r_sigma, margin, out):
                     warm_up()
             for a in range(PACK):
                 square_v(0, a)
-            nc.vector.tensor_scalar(out=two_r[:], in0=r_bf[:], scalar1=2.0, scalar2=None, op0=ALU.mult)
-            nc.vector.tensor_scalar(out=minus_r[:], in0=r_bf[:], scalar1=-1.0, scalar2=None, op0=ALU.mult)
-            nc.vector.tensor_copy(out=m_f[:], in_=m_bf[:])
+            nc.tensor.matmul(wp[:, 0:32], lhsT=ones[:], rhs=rm[:], start=True, stop=True)
             first = [gram_ops(*bank) for bank in banks[:PACK]]
             run(first[0][0])
-            for i in range(5):
+            for i in range(4):
                 norm_step(0, 0, i)
             square_s(0, 4)
-            for a in (5, 6, 7):
-                square_v(0, a)
+            square_v(0, 5)
+            nc.vector.tensor_scalar(out=two_r[:], in0=wp[:, 0:1], scalar1=2.0, scalar2=None, op0=ALU.mult)
+            nc.vector.tensor_scalar(out=minus_r[:], in0=wp[:, 0:1], scalar1=-1.0, scalar2=None, op0=ALU.mult)
+            nc.vector.tensor_copy(out=m_f[:], in_=wp[:, 16:17])
+            norm_step(0, 0, 4)
+            square_v(0, 6)
+            square_v(0, 7)
             norm_rows(0, 0)
             square_s(1, 0)
             run(first[1][0])

@@ -395,7 +395,7 @@ def tile_k_attention_ex_t_kernel(tc, x, r_sigma, margin, out):
                             regroup(b, a, g, nc.vector.tensor_copy)
                     else:
                         regroup(b, a, a // PACK, nc.scalar.copy if a > 5 else nc.vector.tensor_copy)
-                        for q in {4: (4, 5), 5: (6, 7)}.get(a, ()):
+                        for q in {3: (4, 5), 4: (6, 7)}.get(a, ()):
                             regroup(b, q, 0, nc.scalar.copy)
                 if spread:
                     norm_step(prep, 0, sp)

@@ -24,6 +24,8 @@ LEAD = 3
 LEAD_FIRST = 4
 
 WARM = 16
+MIRRORS = {0: (0,), 1: (1,), 2: (2,), 3: (3, 4), 4: (5,), 5: (6,)}
+MIRRORS_LAST = {0: (0,), 1: (1,), 2: (2,), 3: (3, 4), 4: (5, 6)}
 X_SECOND = {-1: (1,), 0: (2,), 1: (3, 4), 2: (5, 6), 3: (7,)}
 AHEAD_2 = {5: (0,), 6: (1,), 7: (2, 3)}
 AHEAD_1 = {0: (4,), 1: (5,), 2: (6,), 3: (7,)}
@@ -365,10 +367,9 @@ def tile_k_attention_ex_t_kernel(tc, x, r_sigma, margin, out):
                 turns = []
                 if prep and cur[1] == 4:
                     turns += [(lambda q: norm_rows(q, 0), prep)]
-                if nxt and nxt < (B - 1, NT - 2):
-                    turns += mirror_ops(*nxt)
-                if nxt == (B - 1, NT - 3):
-                    turns += mirror_ops(B - 1, NT - 2)
+                if nxt:
+                    for a in (MIRRORS if nxt[0] < B - 1 else MIRRORS_LAST).get(nxt[1], ()):
+                        turns += mirror_ops(nxt[0], a)
                 if i in X_SECOND:
                     ahead = [(1, q) for q in X_SECOND[i]]
                 elif prep and prep > 1:

@@ -334,8 +334,6 @@ def tile_k_attention_ex_t_kernel(tc, x, r_sigma, margin, out):
             for g in range(NG):
                 x_regroup(0, g)
                 x_quantize(0, g)
-            square_v(1, 3)
-            square_v(1, 4)
             mask(0, 0)
             done = [PACK]
 
@@ -382,7 +380,7 @@ def tile_k_attention_ex_t_kernel(tc, x, r_sigma, margin, out):
                     ahead += [(cur[0] + 2, q) for q in AHEAD_2.get(cur[1], ())]
                 for b, a in ahead:
                     turns += x_ops(b, a, nc.scalar.copy)
-                goal = min(len(banks), last_bank[tgt] + (LEAD_FIRST if i < 2 else LEAD))
+                goal = min(len(banks), last_bank[tgt] + (LEAD_FIRST if i < 1 else LEAD))
                 products = []
                 while done[0] < goal:
                     chunks, folds = gram_ops(*banks[done[0]])
@@ -416,7 +414,7 @@ def tile_k_attention_ex_t_kernel(tc, x, r_sigma, margin, out):
                     square_s(cur[0] + 2, 2 * cur[1] - NT)
                     square_s(cur[0] + 2, 2 * cur[1] - NT + 1)
                 if i in (-1, 0):
-                    for a in ((5, 6), (7,))[i + 1]:
+                    for a in ((3, 4, 5), (6, 7))[i + 1]:
                         square_v(1, a)
                 if prep and cur[1] in (5, 6):
                     x_regroup(prep, cur[1] - 5)

@@ -25,7 +25,7 @@ LEAD_FIRST = 4
 
 WARM = 16
 MIRRORS = {0: (0,), 1: (1,), 2: (2,), 3: (3, 4), 4: (5,), 5: (6,)}
-MIRRORS_LAST = {0: (0,), 1: (1,), 2: (2,), 3: (3, 4), 4: (5, 6)}
+MIRRORS_LAST = {0: (0,), 1: (1,), 2: (2, 3), 3: (4,), 4: (5, 6)}
 X_SECOND = {-1: (1,), 0: (2,), 1: (3, 4), 2: (5, 6), 3: (7,)}
 AHEAD_2 = {5: (0,), 6: (1,), 7: (2, 3)}
 AHEAD_1 = {0: (4,), 1: (5,), 2: (6,), 3: (7,)}
@@ -273,8 +273,11 @@ def tile_k_attention_ex_t_kernel(tc, x, r_sigma, margin, out):
 
         def finish(b, a):
             res = four.tile([P, C], F32, name="res", tag="res")
-            nc.vector.tensor_tensor(out=res[:], in0=op_of[b, a][:], in1=x_sb[b][:, a, :], op=ALU.add)
-            nc.sync.dma_start(out=out_tok[b, a // PACK, :, a % PACK, :], in_=res[:])
+            w = C // 2 if (b, a) == (B - 1, NT - 1) else C
+            for lo in range(0, C, w):
+                cs = slice(lo, lo + w)
+                nc.vector.tensor_tensor(out=res[:, cs], in0=op_of[b, a][:, cs], in1=x_sb[b][:, a, cs], op=ALU.add)
+                nc.sync.dma_start(out=out_tok[b, a // PACK, :, a % PACK, cs], in_=res[:, cs])
 
         rows = [(b, a) for b in range(B) for a in range(NT)]
         banks = []
@@ -380,7 +383,7 @@ def tile_k_attention_ex_t_kernel(tc, x, r_sigma, margin, out):
                     ahead += [(cur[0] + 2, q) for q in AHEAD_2.get(cur[1], ())]
                 for b, a in ahead:
                     turns += x_ops(b, a, nc.scalar.copy)
-                goal = min(len(banks), last_bank[tgt] + (LEAD_FIRST if i < 1 else LEAD))
+                goal = min(len(banks), last_bank[tgt] + (LEAD_FIRST if i < 1 else LEAD + tgt[0] // (B - 1)))
                 products = []
                 while done[0] < goal:
                     chunks, folds = gram_ops(*banks[done[0]])
@@ -393,8 +396,8 @@ def tile_k_attention_ex_t_kernel(tc, x, r_sigma, margin, out):
                         for g in range(a // PACK + 1):
                             regroup(b, a, g, nc.vector.tensor_copy)
                     else:
-                        regroup(b, a, a // PACK, nc.scalar.copy if a > 5 else nc.vector.tensor_copy)
-                        for q in {3: (4, 5), 4: (6, 7)}.get(a, ()):
+                        regroup(b, a, a // PACK, nc.scalar.copy if a > 6 else nc.vector.tensor_copy)
+                        for q in {3: (4,), 4: (5, 6), 5: (7,)}.get(a, ()):
                             regroup(b, q, 0, nc.scalar.copy)
                 if spread:
                     norm_step(prep, 0, sp)

@@ -340,20 +340,21 @@ def tile_k_attention_ex_t_kernel(tc, x, r_sigma, margin, out):
             mask(0, 0)
             done = [PACK]
 
-            def weave(products, turns):
+            def weave(chunks, folds, turns):
+                products = []
+                for c, f in zip(chunks, folds):
+                    products += [(op, 0) for op in c] + [(op, 1) for op in f]
+                places = sorted(range(len(products) - 1), key=lambda q: products[q][1])[: len(turns)]
                 k = 0
-                for q, op in enumerate(products):
+                for q, (op, narrow) in enumerate(products):
                     run([op])
-                    left = len(products) - 1 - q
-                    while k < len(turns) and left > 0:
+                    if q in places:
                         run([turns[k]])
                         k += 1
-                        if len(turns) - k <= left - 1:
-                            break
                 run(turns[k:])
 
             chunks, folds = gram_ops(*banks[PACK])
-            weave(chunks + folds, x_ops(1, 0, nc.scalar.copy))
+            weave([chunks], [folds], x_ops(1, 0, nc.scalar.copy))
             done[0] += 1
             n = len(rows)
             for i in range(-1, n + 1):
@@ -384,12 +385,9 @@ def tile_k_attention_ex_t_kernel(tc, x, r_sigma, margin, out):
                 for b, a in ahead:
                     turns += x_ops(b, a, nc.scalar.copy)
                 goal = min(len(banks), last_bank[tgt] + (LEAD_FIRST if i < 1 else LEAD + tgt[0] // (B - 1)))
-                products = []
-                while done[0] < goal:
-                    chunks, folds = gram_ops(*banks[done[0]])
-                    products += chunks + folds
-                    done[0] += 1
-                weave(products, turns)
+                ready = [gram_ops(*bank) for bank in banks[done[0] : goal]]
+                done[0] = max(done[0], goal)
+                weave([c for c, f in ready], [f for c, f in ready], turns)
                 if nxt:
                     b, a = nxt
                     if b < B - 1:

@@ -301,11 +301,12 @@ def tile_k_attention_ex_t_kernel(tc, x, r_sigma, margin, out):
 
             for i in range(WARM):
                 warm_up()
+            square_s(0, 0)
             for a in range(NT):
                 for op in x_ops(0, a, nc.scalar.copy):
                     run([op])
                     warm_up()
-            for a in range(PACK):
+            for a in range(1, PACK):
                 square_v(0, a)
             nc.tensor.matmul(wp[:, 0:32], lhsT=ones[:], rhs=rm[:], start=True, stop=True)
             first = [gram_ops(*bank) for bank in banks[:PACK]]

@@ -155,8 +155,8 @@ def tile_k_attention_ex_t_kernel(tc, x, r_sigma, margin, out):
             elif i == 3:
                 nc.vector.tensor_tensor(out=u[:, :, 2], in0=rest, in1=u[:, :, 1], op=ALU.subtract)
             elif i == 4:
-                nc.vector.tensor_scalar(
-                    out=st[b]["bias"][:, cols], in0=sq, scalar1=minus_r[:], scalar2=m_f[:], op0=ALU.mult, op1=ALU.add
+                nc.scalar.activation(
+                    out=st[b]["bias"][:, cols], in_=sq, func=ACT.Identity, bias=m_f[:], scale=minus_r[:]
                 )
 
         def norm_rows(b, half):
@@ -166,10 +166,10 @@ def tile_k_attention_ex_t_kernel(tc, x, r_sigma, margin, out):
             nc.tensor.transpose(tp[:], pieces[b % 2][:], ident[:])
             nc.scalar.copy(out=rt[:], in_=tp[:])
 
-        def x_regroup(b, g):
-            nc.vector.tensor_copy(
-                out=st[b]["xg"][:, g].rearrange("p (c i) j -> p c j i", i=4),
-                in_=x_sb[b][:, PACK * g : PACK * g + PACK, :].rearrange("p j (c i) -> p c j i", i=4),
+        def x_regroup(b, g, copy, cs):
+            copy(
+                out=st[b]["xg"][:, g, cs].rearrange("p (c i) j -> p c j i", i=4),
+                in_=x_sb[b][:, PACK * g : PACK * g + PACK, cs].rearrange("p j (c i) -> p c j i", i=4),
             )
 
         def x_quantize(b, g):
@@ -242,10 +242,11 @@ def tile_k_attention_ex_t_kernel(tc, x, r_sigma, margin, out):
 
             return [(one, s) for s in range(a + 1, NT)]
 
-        def regroup(b, a, g, copy):
+        def regroup(b, a, groups, copy):
+            lo, hi = groups[0], groups[-1] + 1
             copy(
-                out=group(b, a)[:, g],
-                in_=st[b]["kc"][:, PACK * g : PACK * g + PACK, P * a : P * a + P].rearrange("p j t -> p t j"),
+                out=group(b, a)[:, lo:hi],
+                in_=st[b]["kc"][:, PACK * lo : PACK * hi, P * a : P * a + P].rearrange("p (g j) t -> p g t j", j=PACK),
             )
 
         def k_quantize(b, a):
@@ -261,22 +262,30 @@ def tile_k_attention_ex_t_kernel(tc, x, r_sigma, margin, out):
         def multiply(b, a):
             d = st[b]
             kq, ks = codes_of[b, a]
-            op = psum_o.tile([P, C], F32, name="op", tag="o")
-            op_of[b, a] = op
-            for g in range(NG):
-                nc.tensor.matmul_mx(
-                    out=op[:],
-                    lhsT=kq[:, g, :].bitcast(FP8X4), lhsT_scale=ks[:, g, :],
-                    rhs=d["xq"][:, g, :].bitcast(FP8X4), rhs_scale=d["xs"][:, g, :],
-                    start=(g == 0), stop=(g == NG - 1),
-                )
+            halves = 2 if (b, a) >= (B - 1, NT - 2) else 1
+            w = C // halves
+            op_of[b, a] = []
+            for q in range(halves):
+                if halves == 1:
+                    op = psum_o.tile([P, w], F32, name="op", tag="o")
+                else:
+                    op = psum_w.tile([P, w], F32, name="oph", tag="w")
+                op_of[b, a].append(op)
+                cs = slice(w * q, w * q + w)
+                for g in range(NG):
+                    nc.tensor.matmul_mx(
+                        out=op[:],
+                        lhsT=kq[:, g, :].bitcast(FP8X4), lhsT_scale=ks[:, g, :],
+                        rhs=d["xq"][:, g, cs].bitcast(FP8X4), rhs_scale=d["xs"][:, g, cs],
+                        start=(g == 0), stop=(g == NG - 1),
+                    )
 
         def finish(b, a):
             res = four.tile([P, C], F32, name="res", tag="res")
-            w = C // 2 if (b, a) == (B - 1, NT - 1) else C
-            for lo in range(0, C, w):
-                cs = slice(lo, lo + w)
-                nc.vector.tensor_tensor(out=res[:, cs], in0=op_of[b, a][:, cs], in1=x_sb[b][:, a, cs], op=ALU.add)
+            w = C // len(op_of[b, a])
+            for q, op in enumerate(op_of[b, a]):
+                cs = slice(w * q, w * q + w)
+                nc.vector.tensor_tensor(out=res[:, cs], in0=op[:], in1=x_sb[b][:, a, cs], op=ALU.add)
                 nc.sync.dma_start(out=out_tok[b, a // PACK, :, a % PACK, cs], in_=res[:, cs])
 
         rows = [(b, a) for b in range(B) for a in range(NT)]
@@ -336,7 +345,7 @@ def tile_k_attention_ex_t_kernel(tc, x, r_sigma, margin, out):
             run(first[2][1])
             run(first[3][1])
             for g in range(NG):
-                x_regroup(0, g)
+                x_regroup(0, g, nc.vector.tensor_copy, slice(0, C))
                 x_quantize(0, g)
             mask(0, 0)
             done = [PACK]
@@ -392,12 +401,13 @@ def tile_k_attention_ex_t_kernel(tc, x, r_sigma, margin, out):
                 if nxt:
                     b, a = nxt
                     if b < B - 1:
-                        for g in range(a // PACK + 1):
-                            regroup(b, a, g, nc.vector.tensor_copy)
+                        regroup(b, a, range((b, a) >= (B - 2, 6), a // PACK + 1), nc.vector.tensor_copy)
+                        if b == B - 2 and a in (5, 6):
+                            regroup(b, a + 1, (0,), nc.scalar.copy)
                     else:
-                        regroup(b, a, a // PACK, nc.scalar.copy if a > 6 else nc.vector.tensor_copy)
+                        regroup(b, a, (a // PACK,), nc.scalar.copy if a > 6 else nc.vector.tensor_copy)
                         for q in {3: (4,), 4: (5, 6), 5: (7,)}.get(a, ()):
-                            regroup(b, q, 0, nc.scalar.copy)
+                            regroup(b, q, (0,), nc.scalar.copy)
                 if spread:
                     norm_step(prep, 0, sp)
                 if i + 2 < n:
@@ -415,10 +425,15 @@ def tile_k_attention_ex_t_kernel(tc, x, r_sigma, margin, out):
                 if cur and cur[1] >= PACK and cur[0] + 2 < B:
                     square_s(cur[0] + 2, 2 * cur[1] - NT)
                     square_s(cur[0] + 2, 2 * cur[1] - NT + 1)
+                if i == 0:
+                    square_s(1, 7)
                 if i in (-1, 0):
-                    for a in ((3, 4, 5), (6, 7))[i + 1]:
+                    for a in ((3, 4), (5, 6))[i + 1]:
                         square_v(1, a)
-                if prep and cur[1] in (5, 6):
-                    x_regroup(prep, cur[1] - 5)
+                if prep == B - 1 and cur[1] in (4, 5):
+                    for q in (2 * cur[1] - 8, 2 * cur[1] - 7):
+                        x_regroup(prep, 0, nc.scalar.copy, slice(P * q, P * q + P))
+                if prep and cur[1] in (5, 6) and (prep, cur[1]) != (B - 1, 5):
+                    x_regroup(prep, cur[1] - 5, nc.vector.tensor_copy, slice(0, C))
                 if prep and cur[1] in (6, 7):
                     x_quantize(prep, cur[1] - 6)

from contextlib import ExitStack

import concourse.mybir as mybir
from concourse.masks import make_identity

BF16 = mybir.dt.bfloat16
F32 = mybir.dt.float32
U32 = mybir.dt.uint32
U8 = mybir.dt.uint8
FP8X4 = mybir.dt.float8_e4m3fn_x4
ALU = mybir.AluOpType
ACT = mybir.ActivationFunctionType
AX = mybir.AxisListType

B, T, C = 4, 1024, 512
P = 128
NT = T // P
KC = C // P
PACK = 4
NG = T // (P * PACK)
BANK = 512
HALVES = (2, 1, 1, 1)
LEAD = 3
LEAD_FIRST = 4

WARM = 16
MIRRORS = {0: (0,), 1: (1,), 2: (2,), 3: (3, 4), 4: (5,), 5: (6,)}
MIRRORS_LAST = {0: (0,), 1: (1,), 2: (2, 3), 3: (4,), 4: (5, 6)}
X_SECOND = {-1: (1,), 0: (2,), 1: (3, 4), 2: (5, 6), 3: (7,)}
AHEAD_2 = {5: (0,), 6: (1,), 7: (2, 3)}
AHEAD_1 = {0: (4,), 1: (5,), 2: (6,), 3: (7,)}

FLOPS = 2 * (2 * B * T * T * C)


def tile_k_attention_ex_t_kernel(tc, x, r_sigma, margin, out):
    nc = tc.nc
    with ExitStack() as ctx:
        const = ctx.enter_context(tc.tile_pool(name="const", bufs=1))
        xin = ctx.enter_context(tc.tile_pool(name="xin", bufs=B))
        two = ctx.enter_context(tc.tile_pool(name="two", bufs=2))
        eight = ctx.enter_context(tc.tile_pool(name="eight", bufs=8))
        four = ctx.enter_context(tc.tile_pool(name="four", bufs=4))
        psum_w = ctx.enter_context(tc.psum_pool(name="psum_w", bufs=6))
        psum_o = ctx.enter_context(tc.psum_pool(name="psum_o", bufs=2))

        zeros = const.tile([P, P], BF16, name="zeros")
        nc.vector.memset(zeros[:], 0.0)
        rm = const.tile([P, 32], BF16, name="rm")
        nc.vector.memset(rm[:], 0.0)

        x_tok = x.rearrange("b (g p j) c -> b g p j c", p=P, j=PACK)
        out_tok = out.rearrange("b (g p j) c -> b g p j c", p=P, j=PACK)
        x_sb = []
        nc.scalar.dma_start(out=rm[0:1, 0:1], in_=r_sigma.rearrange("(a b) -> a b", a=1))
        nc.scalar.dma_start(out=rm[0:1, 16:17], in_=margin.rearrange("(a b) -> a b", a=1))
        for b in range(B):
            xb = xin.tile([P, NT, C], BF16, name="xb", tag="xb")
            for lo, n in ((0, 1), (1, 1), (2, 2), (4, 2), (6, 2)) if b == 0 else ((0, PACK), (PACK, PACK)):
                g, j = divmod(lo, PACK)
                nc.sync.dma_start(out=xb[:, lo : lo + n, :], in_=x_tok[b, g, :, j : j + n, :])
            x_sb.append(xb)

        ident = const.tile([P, P], BF16, name="ident")
        make_identity(nc, ident[:])
        offdiag = const.tile([P, P], BF16, name="offdiag")
        nc.vector.tensor_scalar(out=offdiag[:], in0=ident[:], scalar1=-1.0, scalar2=1.0, op0=ALU.mult, op1=ALU.add)
        ones = const.tile([P, P], BF16, name="ones")
        nc.vector.memset(ones[:], 1.0)
        warm = const.tile([P, 1], F32, name="warm")
        nc.scalar.activation(out=warm[:], in_=ones[:, 0:1], func=ACT.Exp)
        pieces = []
        for i in range(2):
            u = const.tile([P, P], BF16, name="u%d" % i)
            nc.vector.memset(u[:], 0.0)
            pieces.append(u)
        rowsum = const.tile([P, NT], F32, name="rowsum")
        nc.vector.tensor_reduce(
            out=rowsum[:], in_=ident[:, 0 : 3 * NT].rearrange("p (a i) -> p a i", i=3), axis=AX.X, op=ALU.add
        )
        pick = const.tile([P, NT, P], BF16, name="pick")
        nc.vector.tensor_scalar(
            out=pick[:], in0=rowsum[:].unsqueeze(2).to_broadcast([P, NT, P]), scalar1=-0.5, scalar2=None, op0=ALU.mult
        )

        two_r = const.tile([P, 1], F32, name="two_r")
        minus_r = const.tile([P, 1], F32, name="minus_r")
        m_f = const.tile([P, 1], F32, name="m_f")
        sq_of = []
        for b in range(B):
            sq = const.tile([P, NT], F32, name="sq%d" % b)
            sq_of.append(sq)
        st = {}

        def alloc(b):
            st[b] = {
                "rest": two.tile([P, NT], F32, name="rest", tag="rest"),
                "bias": two.tile([P, NT], F32, name="bias", tag="bias"),
                "xg": two.tile([P, NG, C, PACK], BF16, name="xg", tag="xg", align_bytes=64),
                "xq": two.tile([P, NG, C], U32, name="xq", tag="xq", align_bytes=256),
                "xs": two.tile([P, NG, C], U8, name="xs", tag="xs", align_bytes=256),
                "kc": two.tile([P, NT, T], BF16, name="kc", tag="kc"),
            }

        xT_of = {}

        def alloc_xT(b):
            xT_of[b] = two.tile([P, KC, T], BF16, name="xT", tag="xT")

        def square_s(b, a):
            junk = two.tile([P, C], BF16, name="junk", tag="junk")
            nc.scalar.activation(
                out=junk[:], in_=x_sb[b][:, a, :], func=ACT.Square, accum_out=sq_of[b][:, a : a + 1]
            )

        def square_v(b, a):
            junk = two.tile([P, C], F32, name="junkv", tag="junkv")
            nc.vector.scalar_tensor_tensor(
                out=junk[:], in0=x_sb[b][:, a, :], scalar=1.0, in1=x_sb[b][:, a, :],
                op0=ALU.mult, op1=ALU.mult, accum_out=sq_of[b][:, a : a + 1],
            )

        def x_ops(b, a, copy):
            box = []

            def one(k):
                if k == 0:
                    tp = psum_w.tile([P, KC, P], BF16, name="tp", tag="w")
                    box.append(tp)
                tp = box[0]
                nc.tensor.transpose(tp[:, k, :], x_sb[b][:, a, P * k : P * k + P], ident[:])
                if k == KC - 1:
                    copy(out=xT_of[b][:, :, P * a : P * a + P], in_=tp[:])

            return [(one, k) for k in range(KC)]

        def run(ops):
            for f, q in ops:
                f(q)

        rows_of = {}

        def norm_step(b, half, i):
            n = NT // HALVES[b]
            cols = slice(n * half, n * half + n)
            sq = sq_of[b][:, cols]
            u = pieces[b % 2][:, 0 : 3 * NT].rearrange("p (a i) -> p a i", i=3)[:, cols]
            rest = st[b]["rest"][:, cols]
            if i == 0:
                nc.vector.tensor_copy(out=u[:, :, 0], in_=sq)
            elif i == 1:
                nc.vector.tensor_tensor(out=u[:, :, 1], in0=sq, in1=u[:, :, 0], op=ALU.subtract)
            elif i == 2:
                nc.vector.tensor_tensor(out=rest, in0=sq, in1=u[:, :, 0], op=ALU.subtract)
            elif i == 3:
                nc.vector.tensor_tensor(out=u[:, :, 2], in0=rest, in1=u[:, :, 1], op=ALU.subtract)
            elif i == 4:
                nc.scalar.activation(
                    out=st[b]["bias"][:, cols], in_=sq, func=ACT.Identity, bias=m_f[:], scale=minus_r[:]
                )

        def norm_rows(b, half):
            rt = two.tile([P, P], BF16, name="rows%d" % half, tag="rows%d" % half)
            rows_of[b, half] = rt
            tp = psum_w.tile([P, P], BF16, name="tpr", tag="w")
            nc.tensor.transpose(tp[:], pieces[b % 2][:], ident[:])
            nc.scalar.copy(out=rt[:], in_=tp[:])

        def x_regroup(b, g, copy, cs):
            copy(
                out=st[b]["xg"][:, g, cs].rearrange("p (c i) j -> p c j i", i=4),
                in_=x_sb[b][:, PACK * g : PACK * g + PACK, cs].rearrange("p j (c i) -> p c j i", i=4),
            )

        def x_quantize(b, g):
            d = st[b]
            nc.vector.quantize_mx(
                out=d["xq"][:, g, :].bitcast(FP8X4),
                scales=d["xs"][:, g, :],
                in_=d["xg"][:, g].rearrange("p c j -> p (c j)"),
            )

        def gram_ops(b, a, c0, w):
            box = []

            def chunk(k):
                xT = xT_of[b]
                if k == 0:
                    gp = psum_w.tile([P, BANK], F32, name="gp", tag="w")
                    box.append(gp)
                gp = box[0]
                nc.tensor.matmul(
                    gp[:, :w], lhsT=xT[:, k, P * a : P * a + P], rhs=xT[:, k, c0 : c0 + w], start=(k == 0), stop=False
                )

            def norm(i):
                d = st[b]
                gp = box[0]
                last = i == w // P - 1
                nc.tensor.matmul(
                    gp[:, P * i : P * i + P], lhsT=pick[:, c0 // P + i, :],
                    rhs=rows_of[b, min(c0 // BANK, HALVES[b] - 1)][:], start=False, stop=last,
                )
                if last:
                    nc.scalar.activation(
                        out=d["kc"][:, a, c0 : c0 + w], in_=gp[:, :w], func=ACT.Exp,
                        bias=d["bias"][:, a : a + 1], scale=two_r[:],
                    )

            return [(chunk, k) for k in range(KC)], [(norm, i) for i in range(w // P)]

        def mask(b, a):
            blk = st[b]["kc"][:, a, P * a : P * a + P]
            nc.vector.tensor_tensor(out=blk, in0=blk, in1=offdiag[:], op=ALU.mult)

        grp_of, codes_of, op_of = {}, {}, {}

        def group(b, a):
            if (b, a) not in grp_of:
                grp_of[b, a] = eight.tile([P, NG, P, PACK], BF16, name="grp", tag="grp", align_bytes=64)
            return grp_of[b, a]

        def mirror_ops(b, a):
            kc, lo = st[b]["kc"], P * a
            if a == NT - 1:
                return []
            end = PACK * (a // PACK) + PACK
            box = []

            def one(s):
                if s == a + 1:
                    kt = psum_w.tile([P, NT, P], BF16, name="kt", tag="w")
                    box.append(kt)
                kt = box[0]
                nc.tensor.transpose(kt[:, s, :], kc[:, a, P * s : P * s + P], ident[:])
                if s == end - 1 and a + 1 < end and end == NT:
                    nc.scalar.copy(out=kc[:, a + 1 : end, lo : lo + P], in_=kt[:, a + 1 : end, :])
                if s == NT - 1 and end < NT:
                    if a + 1 < end:
                        nc.scalar.copy(out=kc[:, a + 1 : end, lo : lo + P], in_=kt[:, a + 1 : end, :])
                    nc.scalar.copy(out=group(b, a)[:, 1], in_=kt[:, end:NT, :].rearrange("p j t -> p t j"))

            return [(one, s) for s in range(a + 1, NT)]

        def regroup(b, a, groups, copy):
            lo, hi = groups[0], groups[-1] + 1
            copy(
                out=group(b, a)[:, lo:hi],
                in_=st[b]["kc"][:, PACK * lo : PACK * hi, P * a : P * a + P].rearrange("p (g j) t -> p g t j", j=PACK),
            )

        def k_quantize(b, a):
            kq = four.tile([P, NG, P], U32, name="kq", tag="kq", align_bytes=256)
            ks = four.tile([P, NG, P], U8, name="ks", tag="ks", align_bytes=256)
            codes_of[b, a] = (kq, ks)
            nc.vector.quantize_mx(
                out=kq[:].rearrange("p g t -> p (g t)").bitcast(FP8X4),
                scales=ks[:].rearrange("p g t -> p (g t)"),
                in_=grp_of[b, a][:].rearrange("p g t j -> p (g t j)"),
            )

        def multiply(b, a):
            d = st[b]
            kq, ks = codes_of[b, a]
            halves = 2 if (b, a) >= (B - 1, NT - 2) else 1
            w = C // halves
            op_of[b, a] = []
            for q in range(halves):
                if halves == 1:
                    op = psum_o.tile([P, w], F32, name="op", tag="o")
                else:
                    op = psum_w.tile([P, w], F32, name="oph", tag="w")
                op_of[b, a].append(op)
                cs = slice(w * q, w * q + w)
                for g in range(NG):
                    nc.tensor.matmul_mx(
                        out=op[:],
                        lhsT=kq[:, g, :].bitcast(FP8X4), lhsT_scale=ks[:, g, :],
                        rhs=d["xq"][:, g, cs].bitcast(FP8X4), rhs_scale=d["xs"][:, g, cs],
                        start=(g == 0), stop=(g == NG - 1),
                    )

        def finish(b, a):
            res = four.tile([P, C], F32, name="res", tag="res")
            w = C // len(op_of[b, a])
            for q, op in enumerate(op_of[b, a]):
                cs = slice(w * q, w * q + w)
                nc.vector.tensor_tensor(out=res[:, cs], in0=op[:], in1=x_sb[b][:, a, cs], op=ALU.add)
                nc.sync.dma_start(out=out_tok[b, a // PACK, :, a % PACK, cs], in_=res[:, cs])

        rows = [(b, a) for b in range(B) for a in range(NT)]
        banks = []
        for a in (0, 2):
            banks += [(0, q, P * q, BANK - P * q) for q in (a, a + 1)] + [(0, q, BANK, BANK) for q in (a, a + 1)]
        banks += [(0, a, P * a, T - P * a) for a in range(PACK, NT)]
        banks += [(b, a, c0, min(BANK, T - c0)) for b, a in rows if b for c0 in range(P * a, T, BANK)]
        last_bank = {}
        for i, (b, a, c0, w) in enumerate(banks):
            last_bank[b, a] = i + 1

        with ExitStack() as pinned:
            pinned.enter_context(tc.manual_schedule())
            alloc(0)
            alloc_xT(0)
            alloc_xT(1)
            wp = psum_o.tile([P, BANK], F32, name="wp", tag="o")

            def warm_up():
                nc.tensor.matmul(wp[:, 0:P], lhsT=zeros[:], rhs=zeros[:], start=True, stop=True)

            for i in range(WARM):
                warm_up()
            square_s(0, 0)
            for a in range(NT):
                for op in x_ops(0, a, nc.scalar.copy):
                    run([op])
                    warm_up()
            for a in range(1, PACK):
                square_v(0, a)
            nc.tensor.matmul(wp[:, 0:32], lhsT=ones[:], rhs=rm[:], start=True, stop=True)
            first = [gram_ops(*bank) for bank in banks[:PACK]]
            run(first[0][0])
            for i in range(4):
                norm_step(0, 0, i)
            square_s(0, 4)
            square_v(0, 5)
            nc.vector.tensor_scalar(out=two_r[:], in0=wp[:, 0:1], scalar1=2.0, scalar2=None, op0=ALU.mult)
            nc.vector.tensor_scalar(out=minus_r[:], in0=wp[:, 0:1], scalar1=-1.0, scalar2=None, op0=ALU.mult)
            nc.vector.tensor_copy(out=m_f[:], in_=wp[:, 16:17])
            norm_step(0, 0, 4)
            square_v(0, 6)
            square_v(0, 7)
            norm_rows(0, 0)
            square_s(1, 0)
            run(first[1][0])
            for i in range(5):
                norm_step(0, 1, i)
            run(first[0][1])
            run(first[1][1])
            run(first[2][0])
            norm_rows(0, 1)
            square_s(1, 1)
            square_s(1, 2)
            run(first[3][0])
            run(first[2][1])
            run(first[3][1])
            for g in range(NG):
                x_regroup(0, g, nc.vector.tensor_copy, slice(0, C))
                x_quantize(0, g)
            mask(0, 0)
            done = [PACK]

            def weave(chunks, folds, turns):
                products = []
                for c, f in zip(chunks, folds):
                    products += [(op, 0) for op in c] + [(op, 1) for op in f]
                places = sorted(range(len(products) - 1), key=lambda q: products[q][1])[: len(turns)]
                k = 0
                for q, (op, narrow) in enumerate(products):
                    run([op])
                    if q in places:
                        run([turns[k]])
                        k += 1
                run(turns[k:])

            chunks, folds = gram_ops(*banks[PACK])
            weave([chunks], [folds], x_ops(1, 0, nc.scalar.copy))
            done[0] += 1
            n = len(rows)
            for i in range(-1, n + 1):
                cur = rows[i] if 0 <= i < n else None
                nxt = rows[i + 1] if i + 1 < n else None
                tgt = nxt if nxt else rows[-1]
                prep = cur[0] + 1 if cur and cur[0] + 1 < B else None
                if prep and cur[1] == 0:
                    alloc(prep)
                spread = prep and cur[1] in (1, 2)
                sp = 3 * cur[1] - 3 if spread else 0
                turns = []
                if prep and cur[1] == 4:
                    turns += [(lambda q: norm_rows(q, 0), prep)]
                if nxt:
                    for a in (MIRRORS if nxt[0] < B - 1 else MIRRORS_LAST).get(nxt[1], ()):
                        turns += mirror_ops(nxt[0], a)
                if i in X_SECOND:
                    ahead = [(1, q) for q in X_SECOND[i]]
                elif prep and prep > 1:
                    ahead = [(prep, q) for q in AHEAD_1.get(cur[1], ())]
                else:
                    ahead = []
                if cur and cur[0] + 2 < B:
                    if cur[1] == 5:
                        alloc_xT(cur[0] + 2)
                    ahead += [(cur[0] + 2, q) for q in AHEAD_2.get(cur[1], ())]
                for b, a in ahead:
                    turns += x_ops(b, a, nc.scalar.copy)
                goal = min(len(banks), last_bank[tgt] + (LEAD_FIRST if i < 1 else LEAD + tgt[0] // (B - 1)))
                ready = [gram_ops(*bank) for bank in banks[done[0] : goal]]
                done[0] = max(done[0], goal)
                weave([c for c, f in ready], [f for c, f in ready], turns)
                if nxt:
                    b, a = nxt
                    if b < B - 1:
                        regroup(b, a, range((b, a) >= (B - 2, 6), a // PACK + 1), nc.vector.tensor_copy)
                        if b == B - 2 and a in (5, 6):
                            regroup(b, a + 1, (0,), nc.scalar.copy)
                    else:
                        regroup(b, a, (a // PACK,), nc.scalar.copy if a > 6 else nc.vector.tensor_copy)
                        for q in {3: (4,), 4: (5, 6), 5: (7,)}.get(a, ()):
                            regroup(b, q, (0,), nc.scalar.copy)
                if spread:
                    norm_step(prep, 0, sp)
                if i + 2 < n:
                    mask(*rows[i + 2])
                if i >= 1:
                    finish(*rows[i - 1])
                if spread:
                    norm_step(prep, 0, sp + 1)
                if nxt:
                    k_quantize(*nxt)
                if spread:
                    norm_step(prep, 0, sp + 2)
                if cur:
                    multiply(*cur)
                if cur and cur[1] >= PACK and cur[0] + 2 < B:
                    square_s(cur[0] + 2, 2 * cur[1] - NT)
                    square_s(cur[0] + 2, 2 * cur[1] - NT + 1)
                if i == 0:
                    square_s(1, 7)
                if i in (-1, 0):
                    for a in ((3, 4), (5, 6))[i + 1]:
                        square_v(1, a)
                if prep == B - 1 and cur[1] in (4, 5):
                    for q in (2 * cur[1] - 8, 2 * cur[1] - 7):
                        x_regroup(prep, 0, nc.scalar.copy, slice(P * q, P * q + P))
                if prep and cur[1] in (5, 6) and (prep, cur[1]) != (B - 1, 5):
                    x_regroup(prep, cur[1] - 5, nc.vector.tensor_copy, slice(0, C))
                if prep and cur[1] in (6, 7):
                    x_quantize(prep, cur[1] - 6)
